import numpy as np
import ml_dtypes


def mxq(x, axis, fmt="e4m3"):
    dtype, down = {"e4m3": (ml_dtypes.float8_e4m3fn, 7), "e5m2": (ml_dtypes.float8_e5m2, 14)}[fmt]
    v = np.moveaxis(np.asarray(x, np.float32).astype(ml_dtypes.bfloat16).astype(np.float64), axis, -1)
    blocks = v.reshape(v.shape[:-1] + (-1, 32))
    amax = np.abs(blocks).max(-1, keepdims=True)
    byte = np.maximum(np.where(amax > 0, np.frexp(amax)[1] - 1 + 127, 0) - down, 1)
    scale = np.exp2(byte - 127.0)
    codes = (blocks / scale).astype(np.float32).astype(dtype).astype(np.float64)
    return np.moveaxis((codes * scale).reshape(v.shape), -1, axis)


WIDE = False


def mx_kscale(k):
    if not WIDE:
        return np.ones(k)
    levels = np.array([10, -10, 5, -5, 0])
    a = np.random.permutation(np.resize(levels, k // 512 * 4)).reshape(k // 512, 4)
    idx = np.arange(k)
    return np.exp2(a[idx // 512, idx % 128 // 32])


BF16 = ml_dtypes.bfloat16


def bf(x):
    return np.asarray(x, np.float32).astype(BF16)


def f64(x):
    return np.asarray(x).astype(np.float64)


B, S, HID, H, R, VR, KVR, QLR, HD = 4, 1024, 512, 2, 64, 64, 256, 1024, 128
ROPE_BASE = 10000.0


def rotate_half(x):
    half = x.shape[-1] // 2
    return np.concatenate([-x[..., half:], x[..., :half]], axis=-1)


def rope_tables():
    inv_freq = 1.0 / ROPE_BASE ** (np.arange(0, R, 2) / R)
    freqs = np.outer(np.arange(S), inv_freq)
    emb = np.concatenate([freqs, freqs], axis=-1)
    return np.broadcast_to(np.cos(emb), (B, S, R)), np.broadcast_to(np.sin(emb), (B, S, R))


def setup_inputs():
    s, t = mx_kscale(HID), mx_kscale(QLR)
    cos, sin = rope_tables()
    return {"hidden_states": bf(np.random.standard_normal((B, S, HID)) * s),
            "cos": bf(cos), "sin": bf(sin),
            "w_qa": bf(np.random.standard_normal((QLR, HID)) / np.sqrt(HID) * t[:, None] / s[None, :]),
            "w_qb": bf(np.random.standard_normal((H * (R + KVR), QLR)) / np.sqrt(QLR) / t[None, :]),
            "w_kv": bf(np.random.standard_normal((R + VR + KVR, HID)) / np.sqrt(HID) / s[None, :])}


def reference(hidden_states, cos, sin, w_qa, w_qb, w_kv):
    c, sn = f64(cos), f64(sin)
    hq = mxq(f64(hidden_states), 2, "e4m3")
    q_lora = hq @ mxq(f64(w_qa), 1, "e4m3").T
    q = (mxq(q_lora, 2, "e4m3") @ mxq(f64(w_qb), 1, "e4m3").T).reshape(B, S, H, R + KVR)
    kv = hq @ mxq(f64(w_kv), 1, "e4m3").T
    q_rope = q[..., :R].transpose(0, 2, 1, 3)
    q_rope = q_rope * c[:, None] + rotate_half(q_rope) * sn[:, None]
    q_nope = q[..., R:].transpose(0, 2, 1, 3)
    k_rope = kv[..., :R]
    k_rope = k_rope * c + rotate_half(k_rope) * sn
    v_rope = kv[..., R:R + VR]
    kv_nope = kv[..., R + VR:]
    return q_rope, q_nope, k_rope, v_rope, kv_nope

@@ -1,0 +1,338 @@
+from contextlib import ExitStack
+
+import concourse.mybir as mybir
+from concourse.masks import make_identity
+
+F32 = mybir.dt.float32
+BF16 = mybir.dt.bfloat16
+U32 = mybir.dt.uint32
+U8 = mybir.dt.uint8
+FP8X4 = mybir.dt.float8_e4m3fn_x4
+MULT = mybir.AluOpType.mult
+ADD = mybir.AluOpType.add
+
+P = 128
+TOKENS = 4096
+HID = 512
+QLR = 1024
+STEPS = 32
+CHUNKS = 8
+LAG = 4
+FLOPS = 2 * TOKENS * (HID * QLR + QLR * 640 + HID * 384)
+
+
+def tile_absorbqkvo_pa_t_kernel(
+    tc, hidden_states, cos, sin, w_qa, w_qb, w_kv, out_0, out_1, out_2, out_3, out_4
+):
+    nc = tc.nc
+    hflat = hidden_states.flatten_outer_dims()
+    cosf = cos.flatten_outer_dims()
+    sinf = sin.flatten_outer_dims()
+
+    with ExitStack() as ctx:
+        const = ctx.enter_context(tc.tile_pool(name="const", bufs=1))
+        hpool = ctx.enter_context(tc.tile_pool(name="hpool", bufs=CHUNKS))
+        hgp = ctx.enter_context(tc.tile_pool(name="hgp", bufs=2))
+        hcp = ctx.enter_context(tc.tile_pool(name="hcp", bufs=4))
+        qlgp = ctx.enter_context(tc.tile_pool(name="qlgp", bufs=4))
+        qlcp = ctx.enter_context(tc.tile_pool(name="qlcp", bufs=8))
+        outp = ctx.enter_context(tc.tile_pool(name="outp", bufs=3))
+        tmpp = ctx.enter_context(tc.tile_pool(name="tmpp", bufs=3))
+        psum = ctx.enter_context(tc.psum_pool(name="psum", bufs=8))
+
+        def evac(eng, out, in_):
+            if eng == "s":
+                nc.scalar.copy(out=out, in_=in_)
+            else:
+                nc.vector.tensor_copy(out=out, in_=in_)
+
+        ident = const.tile([P, P], F32, name="ident", tag="ident")
+        make_identity(nc, ident[:])
+
+        h_sb = []
+        for c in range(CHUNKS):
+            h_sb.append(hpool.tile([P, 2048], BF16, name="h_sb", tag="h_sb"))
+
+        def load_h(c):
+            nc.sync.dma_start(
+                out=h_sb[c][:],
+                in_=hflat[512 * c : 512 * (c + 1), :].rearrange("(p j) k -> p (j k)", j=4),
+            )
+
+        wqa_sb = const.tile([P, 4096], BF16, name="wqa_sb", tag="wqa_sb")
+        wkv_sb = const.tile([P, 1536], BF16, name="wkv_sb", tag="wkv_sb")
+        wqb_sb = const.tile([P, 5120], BF16, name="wqb_sb", tag="wqb_sb")
+        cos_sb = const.tile([P, STEPS, 64], BF16, name="cos_sb", tag="cos_sb")
+        sin_sb = const.tile([P, STEPS, 64], BF16, name="sin_sb", tag="sin_sb")
+        ssw_sb = const.tile([P, STEPS, 64], BF16, name="ssw_sb", tag="ssw_sb")
+
+        load_h(0)
+        wqa_src = w_qa.rearrange("(m r e) k -> r m (e k)", m=4, r=P, e=2)
+        wqa_dst = wqa_sb[:].rearrange("p (m x) -> p m x", m=4)
+        nc.sync.dma_start(out=wqa_dst[:, 0:2, :], in_=wqa_src[:, 0:2, :])
+        nc.sync.dma_start(out=wqa_dst[:, 2:4, :], in_=wqa_src[:, 2:4, :])
+        nc.sync.dma_start(
+            out=wkv_sb[:].rearrange("p (a k) -> p a k", a=3),
+            in_=w_kv.rearrange("(a r) k -> r a k", a=3),
+        )
+        wqb_dst = wqb_sb[:].rearrange("p (a k) -> p a k", a=5)
+        for h in range(2):
+            nc.sync.dma_start(
+                out=wqb_dst[:, 2 * h : 2 * h + 2, :],
+                in_=w_qb[320 * h + 64 : 320 * h + 320, :].rearrange("(a r) k -> r a k", a=2),
+            )
+        for h in range(2):
+            nc.sync.dma_start(
+                out=wqb_sb[64 * h : 64 * h + 64, 4096:5120],
+                in_=w_qb[320 * h : 320 * h + 64, :],
+            )
+        load_h(1)
+        nc.sync.dma_start(
+            out=cos_sb[:].rearrange("p (c j) f -> p c (j f)", j=4),
+            in_=cosf.rearrange("(c p j) f -> p c (j f)", c=CHUNKS, p=P, j=4),
+        )
+        nc.sync.dma_start(
+            out=sin_sb[:].rearrange("p (c j) f -> p c (j f)", j=4),
+            in_=sinf.rearrange("(c p j) f -> p c (j f)", c=CHUNKS, p=P, j=4),
+        )
+        for c in range(2, CHUNKS):
+            load_h(c)
+
+        nc.gpsimd.tensor_scalar(
+            out=ssw_sb[:, :, 0:32], in0=sin_sb[:, :, 32:64], scalar1=1.0, scalar2=0.0, op0=MULT, op1=ADD
+        )
+        nc.gpsimd.tensor_scalar(
+            out=ssw_sb[:, :, 32:64], in0=sin_sb[:, :, 0:32], scalar1=-1.0, scalar2=0.0, op0=MULT, op1=ADD
+        )
+
+        def transpose_block(src_words, offsets, dst, eng):
+            n = len(offsets) // 2
+            bank = psum.tile([P, 512], F32, name="bank", tag="bank")
+            for i, off in enumerate(offsets):
+                nc.tensor.transpose(bank[:, i * P : (i + 1) * P], src_words[:, off : off + P], ident[:])
+            evac(eng, dst, bank[:, 0 : n * 256].rearrange("p (a u r) -> p a r u", a=n, u=2))
+
+        hc = {}
+        hs = {}
+        hg = {}
+
+        def tr_h(c):
+            g = hgp.tile([P, 2048], BF16, name="hg", tag="hg", align_bytes=64)
+            hg[c] = g
+            gv = g[:].bitcast(F32).rearrange("p (j r u) -> p j r u", j=4, u=2)
+            words = h_sb[c][:].bitcast(F32)
+            for b in range(2):
+                offs = [256 * (2 * b + a) + P * u for a in range(2) for u in range(2)]
+                transpose_block(words, offs, gv[:, 2 * b : 2 * b + 2], "v" if b == 0 else "s")
+
+        def q_h(c):
+            hc[c] = hcp.tile([P, 512], U32, name="hc", tag="hc", align_bytes=64)
+            hs[c] = hcp.tile([P, 512], U8, name="hs", tag="hs", align_bytes=64)
+            nc.vector.quantize_mx(out=hc[c][:].bitcast(FP8X4), scales=hs[c][:], in_=hg[c][:])
+
+        wqag = const.tile([P, 4096], BF16, name="wqag", tag="wqag", align_bytes=64)
+        wqac = const.tile([P, 1024], U32, name="wqac", tag="wqac", align_bytes=64)
+        wqas = const.tile([P, 1024], U8, name="wqas", tag="wqas", align_bytes=64)
+
+        def prep_wqa():
+            gv = wqag[:].bitcast(F32).rearrange("p (m r u) -> p m r u", m=8, u=2)
+            words = wqa_sb[:].bitcast(F32)
+            for b in range(4):
+                offs = [256 * (2 * b + a) + P * u for a in range(2) for u in range(2)]
+                transpose_block(words, offs, gv[:, 2 * b : 2 * b + 2], "v" if b % 2 == 0 else "s")
+            for g in range(2):
+                nc.vector.quantize_mx(
+                    out=wqac[:, 512 * g : 512 * (g + 1)].bitcast(FP8X4),
+                    scales=wqas[:, 512 * g : 512 * (g + 1)],
+                    in_=wqag[:, 2048 * g : 2048 * (g + 1)],
+                )
+
+        wkvg = const.tile([P, 1536], BF16, name="wkvg", tag="wkvg", align_bytes=64)
+        wkvc = const.tile([P, 384], U32, name="wkvc", tag="wkvc", align_bytes=64)
+        wkvs = const.tile([P, 384], U8, name="wkvs", tag="wkvs", align_bytes=64)
+
+        def prep_wkv():
+            gv = wkvg[:].bitcast(F32).rearrange("p (a r u) -> p a r u", a=3, u=2)
+            words = wkv_sb[:].bitcast(F32)
+            transpose_block(words, [0, 128, 256, 384], gv[:, 0:2], "v")
+            transpose_block(words, [512, 640], gv[:, 2:3], "s")
+            nc.vector.quantize_mx(
+                out=wkvc[:, 0:128].bitcast(FP8X4), scales=wkvs[:, 0:128], in_=wkvg[:, 0:512]
+            )
+            nc.vector.quantize_mx(
+                out=wkvc[:, 128:384].bitcast(FP8X4), scales=wkvs[:, 128:384], in_=wkvg[:, 512:1536]
+            )
+
+        wqbg = const.tile([P, 4096], BF16, name="wqbg", tag="wqbg", align_bytes=64)
+        wqbc = const.tile([P, 1024], U32, name="wqbc", tag="wqbc", align_bytes=64)
+        wqbs = const.tile([P, 1024], U8, name="wqbs", tag="wqbs", align_bytes=64)
+        wqrg = const.tile([P, 1024], BF16, name="wqrg", tag="wqrg", align_bytes=64)
+        wqrc = const.tile([P, 256], U32, name="wqrc", tag="wqrc", align_bytes=64)
+        wqrs = const.tile([P, 256], U8, name="wqrs", tag="wqrs", align_bytes=64)
+
+        def prep_wqb():
+            gv = wqbg[:].bitcast(F32).rearrange("p (g n u) -> p g n u", g=2, u=2)
+            rv = wqrg[:].bitcast(F32).rearrange("p (g n u) -> p g n u", g=2, u=2)
+            words = wqb_sb[:].bitcast(F32)
+            for rt in range(5):
+                offs = [512 * rt + 256 * g + P * u for g in range(2) for u in range(2)]
+                dst = gv[:, :, P * rt : P * (rt + 1), :] if rt < 4 else rv
+                transpose_block(words, offs, dst, "v" if rt % 2 == 0 else "s")
+            for g in range(2):
+                nc.vector.quantize_mx(
+                    out=wqbc[:, 512 * g : 512 * (g + 1)].bitcast(FP8X4),
+                    scales=wqbs[:, 512 * g : 512 * (g + 1)],
+                    in_=wqbg[:, 2048 * g : 2048 * (g + 1)],
+                )
+            nc.vector.quantize_mx(out=wqrc[:].bitcast(FP8X4), scales=wqrs[:], in_=wqrg[:])
+
+        qlg = {}
+        qlc = {}
+        qls = {}
+
+        def s1(s):
+            c, j = divmod(s, 4)
+            g_t = qlgp.tile([P, 1024], BF16, name="qlg", tag="qlg", align_bytes=64)
+            qlg[s] = g_t
+            gv = g_t[:].rearrange("p (g r t) -> p g r t", g=2, t=4)
+            for g in range(2):
+                bank = psum.tile([P, 512], F32, name="bank", tag="bank")
+                for t in range(4):
+                    m = 4 * g + t
+                    nc.tensor.matmul_mx(
+                        out=bank[:, t * P : (t + 1) * P],
+                        lhsT=wqac[:, m * P : (m + 1) * P].bitcast(FP8X4),
+                        lhsT_scale=wqas[:, m * P : (m + 1) * P],
+                        rhs=hc[c][:, j * P : (j + 1) * P].bitcast(FP8X4),
+                        rhs_scale=hs[c][:, j * P : (j + 1) * P],
+                        start=True,
+                        stop=True,
+                    )
+                eng = "v" if (s % 2 == 1 and g == 1) else "s"
+                evac(eng, gv[:, g], bank[:].rearrange("p (t r) -> p r t", t=4))
+
+        def q_ql(s):
+            qlc[s] = qlcp.tile([P, 256], U32, name="qlc", tag="qlc", align_bytes=64)
+            qls[s] = qlcp.tile([P, 256], U8, name="qls", tag="qls", align_bytes=64)
+            nc.vector.quantize_mx(out=qlc[s][:].bitcast(FP8X4), scales=qls[s][:], in_=qlg[s][:])
+
+        cur = {}
+
+        def s2(o):
+            c, j = divmod(o, 4)
+            jj = o % 2
+            if j == 0:
+                cur["qn"] = outp.tile([P, 2, 4, 256], F32, name="qn", tag="qn")
+                cur["kvn"] = outp.tile([P, 4, 256], F32, name="kvn", tag="kvn")
+                cur["rope"] = outp.tile([P, 3, 4, 64], F32, name="rope", tag="rope")
+                cur["v"] = outp.tile([P, 4, 64], F32, name="v", tag="v")
+            if jj == 0:
+                cur["R"] = psum.tile([P, 2, 256], F32, name="bank", tag="bank")
+                cur["KVN"] = psum.tile([P, 2, 256], F32, name="bank", tag="bank")
+            r_b = cur["R"]
+            kvn_b = cur["KVN"]
+            tok = slice(j * P, (j + 1) * P)
+            nc.tensor.matmul_mx(
+                out=r_b[:, jj, 128:256],
+                lhsT=hc[c][:, tok].bitcast(FP8X4), lhsT_scale=hs[c][:, tok],
+                rhs=wkvc[:, 0:128].bitcast(FP8X4), rhs_scale=wkvs[:, 0:128],
+                start=True, stop=True,
+            )
+            nc.tensor.matmul_mx(
+                out=kvn_b[:, jj, :],
+                lhsT=hc[c][:, tok].bitcast(FP8X4), lhsT_scale=hs[c][:, tok],
+                rhs=wkvc[:, 128:384].bitcast(FP8X4), rhs_scale=wkvs[:, 128:384],
+                start=True, stop=True,
+            )
+            for g in range(2):
+                nc.tensor.matmul_mx(
+                    out=r_b[:, jj, 0:128],
+                    lhsT=qlc[o][:, g * P : (g + 1) * P].bitcast(FP8X4),
+                    lhsT_scale=qls[o][:, g * P : (g + 1) * P],
+                    rhs=wqrc[:, P * g : P * (g + 1)].bitcast(FP8X4),
+                    rhs_scale=wqrs[:, P * g : P * (g + 1)],
+                    start=(g == 0), stop=(g == 1),
+                )
+            q_b = psum.tile([P, 512], F32, name="bank", tag="bank")
+            for g in range(2):
+                nc.tensor.matmul_mx(
+                    out=q_b[:],
+                    lhsT=qlc[o][:, g * P : (g + 1) * P].bitcast(FP8X4),
+                    lhsT_scale=qls[o][:, g * P : (g + 1) * P],
+                    rhs=wqbc[:, 512 * g : 512 * (g + 1)].bitcast(FP8X4),
+                    rhs_scale=wqbs[:, 512 * g : 512 * (g + 1)],
+                    start=(g == 0), stop=(g == 1),
+                )
+            evac("s", cur["qn"][:, :, j, :], q_b[:].rearrange("p (h f) -> p h f", h=2))
+            if jj == 1:
+                j0 = j - 1
+                evac("s", cur["kvn"][:, j0 : j0 + 2, :], kvn_b[:])
+                x = r_b[:, :, 0:192].rearrange("p j (g f) -> p j g f", g=3)
+                t1 = tmpp.tile([P, 2, 3, 64], F32, name="t1", tag="t1")
+                t2 = tmpp.tile([P, 2, 3, 64], F32, name="t2", tag="t2")
+                cv = cos_sb[:, o - 1 : o + 1, :].unsqueeze(2).to_broadcast([P, 2, 3, 64])
+                sv = ssw_sb[:, o - 1 : o + 1, :].unsqueeze(2).to_broadcast([P, 2, 3, 64])
+                nc.vector.tensor_tensor(out=t1[:], in0=x, in1=cv, op=MULT)
+                nc.vector.tensor_tensor(out=t2[:], in0=x, in1=sv, op=MULT)
+                nc.vector.tensor_copy(out=cur["v"][:, j0 : j0 + 2, :], in_=r_b[:, :, 192:256])
+                for half in range(2):
+                    a = slice(32 * half, 32 * half + 32)
+                    b = slice(32 * (1 - half), 32 * (1 - half) + 32)
+                    nc.vector.tensor_tensor(
+                        out=cur["rope"][:, :, j0 : j0 + 2, a],
+                        in0=t1[:, :, :, a].rearrange("p j g i -> p g j i"),
+                        in1=t2[:, :, :, b].rearrange("p j g i -> p g j i"),
+                        op=ADD,
+                    )
+            if j == 3 or (c == CHUNKS - 1 and j == 1):
+                nj = 2 if c == CHUNKS - 1 else 4
+                js = slice(j + 1 - nj, j + 1)
+                bb = c // 2
+                rows = slice(512 * (c % 2), 512 * (c % 2) + 512)
+                nc.sync.dma_start(
+                    out=out_1[bb, :, rows, :].rearrange("h (p j) f -> p h j f", j=4)[:, :, js, :],
+                    in_=cur["qn"][:, :, js, :],
+                )
+                nc.sync.dma_start(
+                    out=out_4[bb, rows, :].rearrange("(p j) f -> p j f", j=4)[:, js, :],
+                    in_=cur["kvn"][:, js, :],
+                )
+                nc.sync.dma_start(
+                    out=out_0[bb, :, rows, :].rearrange("h (p j) f -> p h j f", j=4)[:, :, js, :],
+                    in_=cur["rope"][:, 0:2, js, :],
+                )
+                nc.sync.dma_start(
+                    out=out_2[bb, rows, :].rearrange("(p j) f -> p j f", j=4)[:, js, :],
+                    in_=cur["rope"][:, 2, js, :],
+                )
+                nc.sync.dma_start(
+                    out=out_3[bb, rows, :].rearrange("(p j) f -> p j f", j=4)[:, js, :],
+                    in_=cur["v"][:, js, :],
+                )
+
+        tr_h(0)
+        prep_wqa()
+        q_h(0)
+        prep_wkv()
+        s1(0)
+        s1(1)
+        q_ql(0)
+        prep_wqb()
+        tr_h(1)
+        q_ql(1)
+        s1(2)
+        q_h(1)
+        s1(3)
+        q_ql(2)
+        q_ql(3)
+        for it in range(LAG, STEPS + LAG):
+            nxt = it // 4 + 1
+            if it % 4 == 2 and nxt < CHUNKS:
+                tr_h(nxt)
+            if it < STEPS:
+                s1(it)
+            s2(it - LAG)
+            if it % 4 == 2 and nxt < CHUNKS:
+                q_h(nxt)
+            if it < STEPS:
+                q_ql(it)

@@ -16,8 +16,11 @@ TOKENS = 4096
 HID = 512
 QLR = 1024
 STEPS = 32
+PAIRS = 16
 CHUNKS = 8
-LAG = 4
+PIN = False
+GADD = True
+S1_ON_VECTOR = ((1,1),(2,1),(3,1))
 FLOPS = 2 * TOKENS * (HID * QLR + QLR * 640 + HID * 384)
 
 
@@ -30,12 +33,14 @@ def tile_absorbqkvo_pa_t_kernel(
     sinf = sin.flatten_outer_dims()
 
     with ExitStack() as ctx:
+        if PIN:
+            ctx.enter_context(tc.manual_schedule())
         const = ctx.enter_context(tc.tile_pool(name="const", bufs=1))
         hpool = ctx.enter_context(tc.tile_pool(name="hpool", bufs=CHUNKS))
         hgp = ctx.enter_context(tc.tile_pool(name="hgp", bufs=2))
         hcp = ctx.enter_context(tc.tile_pool(name="hcp", bufs=4))
-        qlgp = ctx.enter_context(tc.tile_pool(name="qlgp", bufs=4))
-        qlcp = ctx.enter_context(tc.tile_pool(name="qlcp", bufs=8))
+        qlgp = ctx.enter_context(tc.tile_pool(name="qlgp", bufs=6))
+        qlcp = ctx.enter_context(tc.tile_pool(name="qlcp", bufs=12))
         outp = ctx.enter_context(tc.tile_pool(name="outp", bufs=3))
         tmpp = ctx.enter_context(tc.tile_pool(name="tmpp", bufs=3))
         psum = ctx.enter_context(tc.psum_pool(name="psum", bufs=8))
@@ -45,6 +50,10 @@ def tile_absorbqkvo_pa_t_kernel(
                 nc.scalar.copy(out=out, in_=in_)
             else:
                 nc.vector.tensor_copy(out=out, in_=in_)
+
+        def new_bank():
+            bank = psum.tile([P, 512], F32, name="bank", tag="bank")
+            return bank
 
         ident = const.tile([P, P], F32, name="ident", tag="ident")
         make_identity(nc, ident[:])
@@ -66,50 +75,55 @@ def tile_absorbqkvo_pa_t_kernel(
         sin_sb = const.tile([P, STEPS, 64], BF16, name="sin_sb", tag="sin_sb")
         ssw_sb = const.tile([P, STEPS, 64], BF16, name="ssw_sb", tag="ssw_sb")
 
+        def load_table(dst, src, part):
+            nc.sync.dma_start(
+                out=dst[:, 16 * part : 16 * (part + 1), :].rearrange("p (c j) f -> p c (j f)", j=4),
+                in_=src[2048 * part : 2048 * (part + 1), :].rearrange("(c p j) f -> p c (j f)", c=4, p=P, j=4),
+            )
+
+        def swap_sin(part):
+            st = slice(16 * part, 16 * (part + 1))
+            nc.gpsimd.tensor_scalar(
+                out=ssw_sb[:, st, 0:32], in0=sin_sb[:, st, 32:64], scalar1=1.0, scalar2=0.0, op0=MULT, op1=ADD
+            )
+            nc.gpsimd.tensor_scalar(
+                out=ssw_sb[:, st, 32:64], in0=sin_sb[:, st, 0:32], scalar1=-1.0, scalar2=0.0, op0=MULT, op1=ADD
+            )
+
         load_h(0)
         wqa_src = w_qa.rearrange("(m r e) k -> r m (e k)", m=4, r=P, e=2)
         wqa_dst = wqa_sb[:].rearrange("p (m x) -> p m x", m=4)
-        nc.sync.dma_start(out=wqa_dst[:, 0:2, :], in_=wqa_src[:, 0:2, :])
-        nc.sync.dma_start(out=wqa_dst[:, 2:4, :], in_=wqa_src[:, 2:4, :])
+        for m in range(4):
+            nc.sync.dma_start(out=wqa_dst[:, m, :], in_=wqa_src[:, m, :])
+        load_h(1)
         nc.sync.dma_start(
             out=wkv_sb[:].rearrange("p (a k) -> p a k", a=3),
             in_=w_kv.rearrange("(a r) k -> r a k", a=3),
         )
-        wqb_dst = wqb_sb[:].rearrange("p (a k) -> p a k", a=5)
-        for h in range(2):
-            nc.sync.dma_start(
-                out=wqb_dst[:, 2 * h : 2 * h + 2, :],
-                in_=w_qb[320 * h + 64 : 320 * h + 320, :].rearrange("(a r) k -> r a k", a=2),
-            )
-        for h in range(2):
-            nc.sync.dma_start(
-                out=wqb_sb[64 * h : 64 * h + 64, 4096:5120],
-                in_=w_qb[320 * h : 320 * h + 64, :],
-            )
-        load_h(1)
         nc.sync.dma_start(
-            out=cos_sb[:].rearrange("p (c j) f -> p c (j f)", j=4),
-            in_=cosf.rearrange("(c p j) f -> p c (j f)", c=CHUNKS, p=P, j=4),
+            out=wqb_sb[:].rearrange("p (a k) -> p a k", a=5),
+            in_=w_qb.rearrange("(a r) k -> r a k", a=5),
         )
-        nc.sync.dma_start(
-            out=sin_sb[:].rearrange("p (c j) f -> p c (j f)", j=4),
-            in_=sinf.rearrange("(c p j) f -> p c (j f)", c=CHUNKS, p=P, j=4),
-        )
-        for c in range(2, CHUNKS):
+        load_table(sin_sb, sinf, 0)
+        load_table(cos_sb, cosf, 0)
+        load_h(2)
+        load_h(3)
+        load_table(sin_sb, sinf, 1)
+        load_table(cos_sb, cosf, 1)
+        for c in range(4, CHUNKS):
             load_h(c)
+        swap_sin(0)
+        swap_sin(1)
 
-        nc.gpsimd.tensor_scalar(
-            out=ssw_sb[:, :, 0:32], in0=sin_sb[:, :, 32:64], scalar1=1.0, scalar2=0.0, op0=MULT, op1=ADD
-        )
-        nc.gpsimd.tensor_scalar(
-            out=ssw_sb[:, :, 32:64], in0=sin_sb[:, :, 0:32], scalar1=-1.0, scalar2=0.0, op0=MULT, op1=ADD
-        )
+        def transposes(src_words, offsets):
+            bank = new_bank()
+            for i, off in enumerate(offsets):
+                nc.tensor.transpose(bank[:, i * P : (i + 1) * P], src_words[:, off : off + P], ident[:])
+            return bank
 
         def transpose_block(src_words, offsets, dst, eng):
             n = len(offsets) // 2
-            bank = psum.tile([P, 512], F32, name="bank", tag="bank")
-            for i, off in enumerate(offsets):
-                nc.tensor.transpose(bank[:, i * P : (i + 1) * P], src_words[:, off : off + P], ident[:])
+            bank = transposes(src_words, offsets)
             evac(eng, dst, bank[:, 0 : n * 256].rearrange("p (a u r) -> p a r u", a=n, u=2))
 
         hc = {}
@@ -134,18 +148,18 @@ def tile_absorbqkvo_pa_t_kernel(
         wqac = const.tile([P, 1024], U32, name="wqac", tag="wqac", align_bytes=64)
         wqas = const.tile([P, 1024], U8, name="wqas", tag="wqas", align_bytes=64)
 
-        def prep_wqa():
+        def prep_wqa(m):
             gv = wqag[:].bitcast(F32).rearrange("p (m r u) -> p m r u", m=8, u=2)
             words = wqa_sb[:].bitcast(F32)
-            for b in range(4):
-                offs = [256 * (2 * b + a) + P * u for a in range(2) for u in range(2)]
-                transpose_block(words, offs, gv[:, 2 * b : 2 * b + 2], "v" if b % 2 == 0 else "s")
-            for g in range(2):
-                nc.vector.quantize_mx(
-                    out=wqac[:, 512 * g : 512 * (g + 1)].bitcast(FP8X4),
-                    scales=wqas[:, 512 * g : 512 * (g + 1)],
-                    in_=wqag[:, 2048 * g : 2048 * (g + 1)],
-                )
+            offs = [256 * (2 * m + a) + P * u for a in range(2) for u in range(2)]
+            transpose_block(words, offs, gv[:, 2 * m : 2 * m + 2], "v" if m % 2 == 0 else "s")
+
+        def q_wqa(m):
+            nc.vector.quantize_mx(
+                out=wqac[:, 256 * m : 256 * (m + 1)].bitcast(FP8X4),
+                scales=wqas[:, 256 * m : 256 * (m + 1)],
+                in_=wqag[:, 1024 * m : 1024 * (m + 1)],
+            )
 
         wkvg = const.tile([P, 1536], BF16, name="wkvg", tag="wkvg", align_bytes=64)
         wkvc = const.tile([P, 384], U32, name="wkvc", tag="wkvc", align_bytes=64)
@@ -154,8 +168,8 @@ def tile_absorbqkvo_pa_t_kernel(
         def prep_wkv():
             gv = wkvg[:].bitcast(F32).rearrange("p (a r u) -> p a r u", a=3, u=2)
             words = wkv_sb[:].bitcast(F32)
-            transpose_block(words, [0, 128, 256, 384], gv[:, 0:2], "v")
-            transpose_block(words, [512, 640], gv[:, 2:3], "s")
+            transpose_block(words, [0, 128, 256, 384], gv[:, 0:2], "s")
+            transpose_block(words, [512, 640], gv[:, 2:3], "v")
             nc.vector.quantize_mx(
                 out=wkvc[:, 0:128].bitcast(FP8X4), scales=wkvs[:, 0:128], in_=wkvg[:, 0:512]
             )
@@ -170,46 +184,58 @@ def tile_absorbqkvo_pa_t_kernel(
         wqrc = const.tile([P, 256], U32, name="wqrc", tag="wqrc", align_bytes=64)
         wqrs = const.tile([P, 256], U8, name="wqrs", tag="wqrs", align_bytes=64)
 
+        WQB_RUNS = (
+            ((0, 64, True, 0), (64, 64, False, 0)),
+            ((0, 128, False, 64),),
+            ((0, 64, False, 192), (64, 64, True, 64)),
+            ((0, 128, False, 256),),
+            ((0, 128, False, 384),),
+        )
+
         def prep_wqb():
             gv = wqbg[:].bitcast(F32).rearrange("p (g n u) -> p g n u", g=2, u=2)
             rv = wqrg[:].bitcast(F32).rearrange("p (g n u) -> p g n u", g=2, u=2)
             words = wqb_sb[:].bitcast(F32)
-            for rt in range(5):
-                offs = [512 * rt + 256 * g + P * u for g in range(2) for u in range(2)]
-                dst = gv[:, :, P * rt : P * (rt + 1), :] if rt < 4 else rv
-                transpose_block(words, offs, dst, "v" if rt % 2 == 0 else "s")
+            for a in range(5):
+                offs = [512 * a + 256 * g + P * u for g in range(2) for u in range(2)]
+                bank = transposes(words, offs)
+                bv = bank[:].rearrange("p (g u r) -> p g r u", g=2, u=2)
+                for r0, nr, rotary, n0 in WQB_RUNS[a]:
+                    dst = rv if rotary else gv
+                    evac("v" if a % 2 == 0 else "s", dst[:, :, n0 : n0 + nr, :], bv[:, :, r0 : r0 + nr, :])
+
+        def q_wqb():
+            nc.vector.quantize_mx(out=wqrc[:].bitcast(FP8X4), scales=wqrs[:], in_=wqrg[:])
             for g in range(2):
                 nc.vector.quantize_mx(
                     out=wqbc[:, 512 * g : 512 * (g + 1)].bitcast(FP8X4),
                     scales=wqbs[:, 512 * g : 512 * (g + 1)],
                     in_=wqbg[:, 2048 * g : 2048 * (g + 1)],
                 )
-            nc.vector.quantize_mx(out=wqrc[:].bitcast(FP8X4), scales=wqrs[:], in_=wqrg[:])
 
         qlg = {}
         qlc = {}
         qls = {}
 
-        def s1(s):
+        def s1_half(s, g):
             c, j = divmod(s, 4)
-            g_t = qlgp.tile([P, 1024], BF16, name="qlg", tag="qlg", align_bytes=64)
-            qlg[s] = g_t
-            gv = g_t[:].rearrange("p (g r t) -> p g r t", g=2, t=4)
-            for g in range(2):
-                bank = psum.tile([P, 512], F32, name="bank", tag="bank")
-                for t in range(4):
-                    m = 4 * g + t
-                    nc.tensor.matmul_mx(
-                        out=bank[:, t * P : (t + 1) * P],
-                        lhsT=wqac[:, m * P : (m + 1) * P].bitcast(FP8X4),
-                        lhsT_scale=wqas[:, m * P : (m + 1) * P],
-                        rhs=hc[c][:, j * P : (j + 1) * P].bitcast(FP8X4),
-                        rhs_scale=hs[c][:, j * P : (j + 1) * P],
-                        start=True,
-                        stop=True,
-                    )
-                eng = "v" if (s % 2 == 1 and g == 1) else "s"
-                evac(eng, gv[:, g], bank[:].rearrange("p (t r) -> p r t", t=4))
+            if s not in qlg:
+                qlg[s] = qlgp.tile([P, 1024], BF16, name="qlg", tag="qlg", align_bytes=64)
+            gv = qlg[s][:].rearrange("p (g r t) -> p g r t", g=2, t=4)
+            bank = new_bank()
+            for t in range(4):
+                m = 4 * g + t
+                nc.tensor.matmul_mx(
+                    out=bank[:, t * P : (t + 1) * P],
+                    lhsT=wqac[:, m * P : (m + 1) * P].bitcast(FP8X4),
+                    lhsT_scale=wqas[:, m * P : (m + 1) * P],
+                    rhs=hc[c][:, j * P : (j + 1) * P].bitcast(FP8X4),
+                    rhs_scale=hs[c][:, j * P : (j + 1) * P],
+                    start=True,
+                    stop=True,
+                )
+            eng = "v" if (j, g) in S1_ON_VECTOR else "s"
+            evac(eng, gv[:, g], bank[:].rearrange("p (t r) -> p r t", t=4))
 
         def q_ql(s):
             qlc[s] = qlcp.tile([P, 256], U32, name="qlc", tag="qlc", align_bytes=64)
@@ -218,121 +244,137 @@ def tile_absorbqkvo_pa_t_kernel(
 
         cur = {}
 
-        def s2(o):
-            c, j = divmod(o, 4)
-            jj = o % 2
-            if j == 0:
+        def out_pair(q):
+            o0 = 2 * q
+            c = o0 // 4
+            j0 = o0 % 4
+            js = slice(j0, j0 + 2)
+            tail = q >= PAIRS - 1
+            bb = c // 2
+            rows = slice(512 * (c % 2), 512 * (c % 2) + 512)
+            if j0 == 0:
                 cur["qn"] = outp.tile([P, 2, 4, 256], F32, name="qn", tag="qn")
                 cur["kvn"] = outp.tile([P, 4, 256], F32, name="kvn", tag="kvn")
                 cur["rope"] = outp.tile([P, 3, 4, 64], F32, name="rope", tag="rope")
-                cur["v"] = outp.tile([P, 4, 64], F32, name="v", tag="v")
-            if jj == 0:
-                cur["R"] = psum.tile([P, 2, 256], F32, name="bank", tag="bank")
-                cur["KVN"] = psum.tile([P, 2, 256], F32, name="bank", tag="bank")
-            r_b = cur["R"]
-            kvn_b = cur["KVN"]
-            tok = slice(j * P, (j + 1) * P)
-            nc.tensor.matmul_mx(
-                out=r_b[:, jj, 128:256],
-                lhsT=hc[c][:, tok].bitcast(FP8X4), lhsT_scale=hs[c][:, tok],
-                rhs=wkvc[:, 0:128].bitcast(FP8X4), rhs_scale=wkvs[:, 0:128],
-                start=True, stop=True,
-            )
-            nc.tensor.matmul_mx(
-                out=kvn_b[:, jj, :],
-                lhsT=hc[c][:, tok].bitcast(FP8X4), lhsT_scale=hs[c][:, tok],
-                rhs=wkvc[:, 128:384].bitcast(FP8X4), rhs_scale=wkvs[:, 128:384],
-                start=True, stop=True,
-            )
-            for g in range(2):
+                cur["v"] = outp.tile([P, 4, 64], F32, name="v_sb", tag="v_sb")
+            qn = cur["qn"]
+            kvn = cur["kvn"]
+            rope = cur["rope"]
+            v_sb = cur["v"]
+            r_b = psum.tile([P, 2, 256], F32, name="bank", tag="bank")
+            kvn_b = psum.tile([P, 2, 256], F32, name="bank", tag="bank")
+            for jj in range(2):
+                tok = slice((j0 + jj) * P, (j0 + jj + 1) * P)
                 nc.tensor.matmul_mx(
-                    out=r_b[:, jj, 0:128],
-                    lhsT=qlc[o][:, g * P : (g + 1) * P].bitcast(FP8X4),
-                    lhsT_scale=qls[o][:, g * P : (g + 1) * P],
-                    rhs=wqrc[:, P * g : P * (g + 1)].bitcast(FP8X4),
-                    rhs_scale=wqrs[:, P * g : P * (g + 1)],
-                    start=(g == 0), stop=(g == 1),
+                    out=r_b[:, jj, 128:256],
+                    lhsT=hc[c][:, tok].bitcast(FP8X4), lhsT_scale=hs[c][:, tok],
+                    rhs=wkvc[:, 0:128].bitcast(FP8X4), rhs_scale=wkvs[:, 0:128],
+                    start=True, stop=True,
                 )
-            q_b = psum.tile([P, 512], F32, name="bank", tag="bank")
-            for g in range(2):
                 nc.tensor.matmul_mx(
-                    out=q_b[:],
-                    lhsT=qlc[o][:, g * P : (g + 1) * P].bitcast(FP8X4),
-                    lhsT_scale=qls[o][:, g * P : (g + 1) * P],
-                    rhs=wqbc[:, 512 * g : 512 * (g + 1)].bitcast(FP8X4),
-                    rhs_scale=wqbs[:, 512 * g : 512 * (g + 1)],
-                    start=(g == 0), stop=(g == 1),
+                    out=kvn_b[:, jj, :],
+                    lhsT=hc[c][:, tok].bitcast(FP8X4), lhsT_scale=hs[c][:, tok],
+                    rhs=wkvc[:, 128:384].bitcast(FP8X4), rhs_scale=wkvs[:, 128:384],
+                    start=True, stop=True,
                 )
-            evac("s", cur["qn"][:, :, j, :], q_b[:].rearrange("p (h f) -> p h f", h=2))
-            if jj == 1:
-                j0 = j - 1
-                evac("s", cur["kvn"][:, j0 : j0 + 2, :], kvn_b[:])
-                x = r_b[:, :, 0:192].rearrange("p j (g f) -> p j g f", g=3)
-                t1 = tmpp.tile([P, 2, 3, 64], F32, name="t1", tag="t1")
-                t2 = tmpp.tile([P, 2, 3, 64], F32, name="t2", tag="t2")
-                cv = cos_sb[:, o - 1 : o + 1, :].unsqueeze(2).to_broadcast([P, 2, 3, 64])
-                sv = ssw_sb[:, o - 1 : o + 1, :].unsqueeze(2).to_broadcast([P, 2, 3, 64])
-                nc.vector.tensor_tensor(out=t1[:], in0=x, in1=cv, op=MULT)
-                nc.vector.tensor_tensor(out=t2[:], in0=x, in1=sv, op=MULT)
-                nc.vector.tensor_copy(out=cur["v"][:, j0 : j0 + 2, :], in_=r_b[:, :, 192:256])
-                for half in range(2):
-                    a = slice(32 * half, 32 * half + 32)
-                    b = slice(32 * (1 - half), 32 * (1 - half) + 32)
-                    nc.vector.tensor_tensor(
-                        out=cur["rope"][:, :, j0 : j0 + 2, a],
-                        in0=t1[:, :, :, a].rearrange("p j g i -> p g j i"),
-                        in1=t2[:, :, :, b].rearrange("p j g i -> p g j i"),
-                        op=ADD,
+            evac("s", kvn[:, js, :], kvn_b[:])
+            for jj in range(2):
+                o = o0 + jj
+                for g in range(2):
+                    nc.tensor.matmul_mx(
+                        out=r_b[:, jj, 0:128],
+                        lhsT=qlc[o][:, g * P : (g + 1) * P].bitcast(FP8X4),
+                        lhsT_scale=qls[o][:, g * P : (g + 1) * P],
+                        rhs=wqrc[:, P * g : P * (g + 1)].bitcast(FP8X4),
+                        rhs_scale=wqrs[:, P * g : P * (g + 1)],
+                        start=(g == 0), stop=(g == 1),
                     )
-            if j == 3 or (c == CHUNKS - 1 and j == 1):
-                nj = 2 if c == CHUNKS - 1 else 4
-                js = slice(j + 1 - nj, j + 1)
-                bb = c // 2
-                rows = slice(512 * (c % 2), 512 * (c % 2) + 512)
+            x = r_b[:, :, 0:192].rearrange("p j (g f) -> p j g f", g=3)
+            t1 = tmpp.tile([P, 2, 3, 64], F32, name="t1", tag="t1")
+            t2 = tmpp.tile([P, 2, 3, 64], F32, name="t2", tag="t2")
+            cv = cos_sb[:, o0 : o0 + 2, :].unsqueeze(2).to_broadcast([P, 2, 3, 64])
+            sv = ssw_sb[:, o0 : o0 + 2, :].unsqueeze(2).to_broadcast([P, 2, 3, 64])
+            nc.vector.tensor_tensor(out=t1[:], in0=x, in1=cv, op=MULT)
+            nc.vector.tensor_tensor(out=t2[:], in0=x, in1=sv, op=MULT)
+            nc.vector.tensor_copy(out=v_sb[:, js, :], in_=r_b[:, :, 192:256])
+            add_eng = nc.gpsimd if (GADD and not tail) else nc.vector
+            for half in range(2):
+                a = slice(32 * half, 32 * half + 32)
+                b = slice(32 * (1 - half), 32 * (1 - half) + 32)
+                add_eng.tensor_tensor(
+                    out=rope[:, :, js, a],
+                    in0=t1[:, :, :, a].rearrange("p j g i -> p g j i"),
+                    in1=t2[:, :, :, b].rearrange("p j g i -> p g j i"),
+                    op=ADD,
+                )
+            qdst = out_1[bb, :, rows, :].rearrange("h (p j) f -> p h j f", j=4)
+            for jj in range(2):
+                o = o0 + jj
+                j = j0 + jj
+                q_b = new_bank()
+                for g in range(2):
+                    nc.tensor.matmul_mx(
+                        out=q_b[:],
+                        lhsT=qlc[o][:, g * P : (g + 1) * P].bitcast(FP8X4),
+                        lhsT_scale=qls[o][:, g * P : (g + 1) * P],
+                        rhs=wqbc[:, 512 * g : 512 * (g + 1)].bitcast(FP8X4),
+                        rhs_scale=wqbs[:, 512 * g : 512 * (g + 1)],
+                        start=(g == 0), stop=(g == 1),
+                    )
+                evac("v" if (tail and jj == 0) else "s", qn[:, :, j, :], q_b[:].rearrange("p (h f) -> p h f", h=2))
+                if tail:
+                    nc.sync.dma_start(out=qdst[:, :, j : j + 1, :], in_=qn[:, :, j : j + 1, :])
+            fine = c == CHUNKS - 1
+            if fine or j0 == 2:
+                sl = js if fine else slice(0, 4)
+                if not tail:
+                    nc.sync.dma_start(out=qdst[:, :, sl, :], in_=qn[:, :, sl, :])
                 nc.sync.dma_start(
-                    out=out_1[bb, :, rows, :].rearrange("h (p j) f -> p h j f", j=4)[:, :, js, :],
-                    in_=cur["qn"][:, :, js, :],
+                    out=out_4[bb, rows, :].rearrange("(p j) f -> p j f", j=4)[:, sl, :], in_=kvn[:, sl, :]
                 )
                 nc.sync.dma_start(
-                    out=out_4[bb, rows, :].rearrange("(p j) f -> p j f", j=4)[:, js, :],
-                    in_=cur["kvn"][:, js, :],
+                    out=out_3[bb, rows, :].rearrange("(p j) f -> p j f", j=4)[:, sl, :], in_=v_sb[:, sl, :]
                 )
                 nc.sync.dma_start(
-                    out=out_0[bb, :, rows, :].rearrange("h (p j) f -> p h j f", j=4)[:, :, js, :],
-                    in_=cur["rope"][:, 0:2, js, :],
+                    out=out_0[bb, :, rows, :].rearrange("h (p j) f -> p h j f", j=4)[:, :, sl, :],
+                    in_=rope[:, 0:2, sl, :],
                 )
                 nc.sync.dma_start(
-                    out=out_2[bb, rows, :].rearrange("(p j) f -> p j f", j=4)[:, js, :],
-                    in_=cur["rope"][:, 2, js, :],
-                )
-                nc.sync.dma_start(
-                    out=out_3[bb, rows, :].rearrange("(p j) f -> p j f", j=4)[:, js, :],
-                    in_=cur["v"][:, js, :],
+                    out=out_2[bb, rows, :].rearrange("(p j) f -> p j f", j=4)[:, sl, :], in_=rope[:, 2, sl, :]
                 )
 
         tr_h(0)
-        prep_wqa()
+        prep_wqa(0)
         q_h(0)
-        prep_wkv()
-        s1(0)
-        s1(1)
-        q_ql(0)
-        prep_wqb()
+        prep_wqa(1)
+        q_wqa(0)
+        prep_wqa(2)
+        q_wqa(1)
+        prep_wqa(3)
+        q_wqa(2)
+        q_wqa(3)
+        for j in range(4):
+            s1_half(j, 0)
         tr_h(1)
-        q_ql(1)
-        s1(2)
-        q_h(1)
-        s1(3)
-        q_ql(2)
-        q_ql(3)
-        for it in range(LAG, STEPS + LAG):
-            nxt = it // 4 + 1
-            if it % 4 == 2 and nxt < CHUNKS:
-                tr_h(nxt)
-            if it < STEPS:
-                s1(it)
-            s2(it - LAG)
-            if it % 4 == 2 and nxt < CHUNKS:
-                q_h(nxt)
-            if it < STEPS:
-                q_ql(it)
+        prep_wkv()
+        for j in range(4):
+            s1_half(j, 1)
+            q_ql(j)
+            if j == 0:
+                q_h(1)
+        prep_wqb()
+        q_wqb()
+        out_pair(0)
+        for q in range(2, PAIRS + 1):
+            if q % 2 == 0 and q // 2 + 1 < CHUNKS:
+                tr_h(q // 2 + 1)
+            if q < PAIRS:
+                for s in (2 * q, 2 * q + 1):
+                    s1_half(s, 0)
+                    s1_half(s, 1)
+            out_pair(q - 1)
+            if q % 2 == 0 and q // 2 + 1 < CHUNKS:
+                q_h(q // 2 + 1)
+            if q < PAIRS:
+                q_ql(2 * q)
+                q_ql(2 * q + 1)

@@ -18,9 +18,8 @@ QLR = 1024
 STEPS = 32
 PAIRS = 16
 CHUNKS = 8
-PIN = False
+PIN = True
 GADD = True
-S1_ON_VECTOR = ((1,1),(2,1),(3,1))
 FLOPS = 2 * TOKENS * (HID * QLR + QLR * 640 + HID * 384)
 
 
@@ -38,9 +37,9 @@ def tile_absorbqkvo_pa_t_kernel(
         const = ctx.enter_context(tc.tile_pool(name="const", bufs=1))
         hpool = ctx.enter_context(tc.tile_pool(name="hpool", bufs=CHUNKS))
         hgp = ctx.enter_context(tc.tile_pool(name="hgp", bufs=2))
-        hcp = ctx.enter_context(tc.tile_pool(name="hcp", bufs=4))
+        hcp = ctx.enter_context(tc.tile_pool(name="hcp", bufs=5))
         qlgp = ctx.enter_context(tc.tile_pool(name="qlgp", bufs=6))
-        qlcp = ctx.enter_context(tc.tile_pool(name="qlcp", bufs=12))
+        qlcp = ctx.enter_context(tc.tile_pool(name="qlcp", bufs=14))
         outp = ctx.enter_context(tc.tile_pool(name="outp", bufs=3))
         tmpp = ctx.enter_context(tc.tile_pool(name="tmpp", bufs=3))
         psum = ctx.enter_context(tc.psum_pool(name="psum", bufs=8))
@@ -62,7 +61,7 @@ def tile_absorbqkvo_pa_t_kernel(
         for c in range(CHUNKS):
             h_sb.append(hpool.tile([P, 2048], BF16, name="h_sb", tag="h_sb"))
 
-        def load_h(c):
+        def loadh(c):
             nc.sync.dma_start(
                 out=h_sb[c][:],
                 in_=hflat[512 * c : 512 * (c + 1), :].rearrange("(p j) k -> p (j k)", j=4),
@@ -81,7 +80,13 @@ def tile_absorbqkvo_pa_t_kernel(
                 in_=src[2048 * part : 2048 * (part + 1), :].rearrange("(c p j) f -> p c (j f)", c=4, p=P, j=4),
             )
 
-        def swap_sin(part):
+        def loadsin(part):
+            load_table(sin_sb, sinf, part)
+
+        def loadcos(part):
+            load_table(cos_sb, cosf, part)
+
+        def swap(part):
             st = slice(16 * part, 16 * (part + 1))
             nc.gpsimd.tensor_scalar(
                 out=ssw_sb[:, st, 0:32], in0=sin_sb[:, st, 32:64], scalar1=1.0, scalar2=0.0, op0=MULT, op1=ADD
@@ -90,30 +95,23 @@ def tile_absorbqkvo_pa_t_kernel(
                 out=ssw_sb[:, st, 32:64], in0=sin_sb[:, st, 0:32], scalar1=-1.0, scalar2=0.0, op0=MULT, op1=ADD
             )
 
-        load_h(0)
         wqa_src = w_qa.rearrange("(m r e) k -> r m (e k)", m=4, r=P, e=2)
         wqa_dst = wqa_sb[:].rearrange("p (m x) -> p m x", m=4)
-        for m in range(4):
+
+        def loadwqa(m):
             nc.sync.dma_start(out=wqa_dst[:, m, :], in_=wqa_src[:, m, :])
-        load_h(1)
-        nc.sync.dma_start(
-            out=wkv_sb[:].rearrange("p (a k) -> p a k", a=3),
-            in_=w_kv.rearrange("(a r) k -> r a k", a=3),
-        )
-        nc.sync.dma_start(
-            out=wqb_sb[:].rearrange("p (a k) -> p a k", a=5),
-            in_=w_qb.rearrange("(a r) k -> r a k", a=5),
-        )
-        load_table(sin_sb, sinf, 0)
-        load_table(cos_sb, cosf, 0)
-        load_h(2)
-        load_h(3)
-        load_table(sin_sb, sinf, 1)
-        load_table(cos_sb, cosf, 1)
-        for c in range(4, CHUNKS):
-            load_h(c)
-        swap_sin(0)
-        swap_sin(1)
+
+        def loadwkv():
+            nc.sync.dma_start(
+                out=wkv_sb[:].rearrange("p (a k) -> p a k", a=3),
+                in_=w_kv.rearrange("(a r) k -> r a k", a=3),
+            )
+
+        def loadwqb():
+            nc.sync.dma_start(
+                out=wqb_sb[:].rearrange("p (a k) -> p a k", a=5),
+                in_=w_qb.rearrange("(a r) k -> r a k", a=5),
+            )
 
         def transposes(src_words, offsets):
             bank = new_bank()
@@ -130,14 +128,14 @@ def tile_absorbqkvo_pa_t_kernel(
         hs = {}
         hg = {}
 
-        def tr_h(c):
+        def tr_h(c, e0, e1):
             g = hgp.tile([P, 2048], BF16, name="hg", tag="hg", align_bytes=64)
             hg[c] = g
             gv = g[:].bitcast(F32).rearrange("p (j r u) -> p j r u", j=4, u=2)
             words = h_sb[c][:].bitcast(F32)
             for b in range(2):
                 offs = [256 * (2 * b + a) + P * u for a in range(2) for u in range(2)]
-                transpose_block(words, offs, gv[:, 2 * b : 2 * b + 2], "v" if b == 0 else "s")
+                transpose_block(words, offs, gv[:, 2 * b : 2 * b + 2], e0 if b == 0 else e1)
 
         def q_h(c):
             hc[c] = hcp.tile([P, 512], U32, name="hc", tag="hc", align_bytes=64)
@@ -148,11 +146,11 @@ def tile_absorbqkvo_pa_t_kernel(
         wqac = const.tile([P, 1024], U32, name="wqac", tag="wqac", align_bytes=64)
         wqas = const.tile([P, 1024], U8, name="wqas", tag="wqas", align_bytes=64)
 
-        def prep_wqa(m):
+        def prep_wqa(m, eng):
             gv = wqag[:].bitcast(F32).rearrange("p (m r u) -> p m r u", m=8, u=2)
             words = wqa_sb[:].bitcast(F32)
             offs = [256 * (2 * m + a) + P * u for a in range(2) for u in range(2)]
-            transpose_block(words, offs, gv[:, 2 * m : 2 * m + 2], "v" if m % 2 == 0 else "s")
+            transpose_block(words, offs, gv[:, 2 * m : 2 * m + 2], eng)
 
         def q_wqa(m):
             nc.vector.quantize_mx(
@@ -165,11 +163,13 @@ def tile_absorbqkvo_pa_t_kernel(
         wkvc = const.tile([P, 384], U32, name="wkvc", tag="wkvc", align_bytes=64)
         wkvs = const.tile([P, 384], U8, name="wkvs", tag="wkvs", align_bytes=64)
 
-        def prep_wkv():
+        def prep_wkv(e0, e1):
             gv = wkvg[:].bitcast(F32).rearrange("p (a r u) -> p a r u", a=3, u=2)
             words = wkv_sb[:].bitcast(F32)
-            transpose_block(words, [0, 128, 256, 384], gv[:, 0:2], "s")
-            transpose_block(words, [512, 640], gv[:, 2:3], "v")
+            transpose_block(words, [0, 128, 256, 384], gv[:, 0:2], e0)
+            transpose_block(words, [512, 640], gv[:, 2:3], e1)
+
+        def q_wkv():
             nc.vector.quantize_mx(
                 out=wkvc[:, 0:128].bitcast(FP8X4), scales=wkvs[:, 0:128], in_=wkvg[:, 0:512]
             )
@@ -192,7 +192,7 @@ def tile_absorbqkvo_pa_t_kernel(
             ((0, 128, False, 384),),
         )
 
-        def prep_wqb():
+        def prep_wqb(engs):
             gv = wqbg[:].bitcast(F32).rearrange("p (g n u) -> p g n u", g=2, u=2)
             rv = wqrg[:].bitcast(F32).rearrange("p (g n u) -> p g n u", g=2, u=2)
             words = wqb_sb[:].bitcast(F32)
@@ -202,10 +202,12 @@ def tile_absorbqkvo_pa_t_kernel(
                 bv = bank[:].rearrange("p (g u r) -> p g r u", g=2, u=2)
                 for r0, nr, rotary, n0 in WQB_RUNS[a]:
                     dst = rv if rotary else gv
-                    evac("v" if a % 2 == 0 else "s", dst[:, :, n0 : n0 + nr, :], bv[:, :, r0 : r0 + nr, :])
+                    evac(engs[a], dst[:, :, n0 : n0 + nr, :], bv[:, :, r0 : r0 + nr, :])
 
-        def q_wqb():
+        def q_wqr():
             nc.vector.quantize_mx(out=wqrc[:].bitcast(FP8X4), scales=wqrs[:], in_=wqrg[:])
+
+        def q_wqn():
             for g in range(2):
                 nc.vector.quantize_mx(
                     out=wqbc[:, 512 * g : 512 * (g + 1)].bitcast(FP8X4),
@@ -217,7 +219,7 @@ def tile_absorbqkvo_pa_t_kernel(
         qlc = {}
         qls = {}
 
-        def s1_half(s, g):
+        def s1_half(s, g, eng):
             c, j = divmod(s, 4)
             if s not in qlg:
                 qlg[s] = qlgp.tile([P, 1024], BF16, name="qlg", tag="qlg", align_bytes=64)
@@ -234,7 +236,6 @@ def tile_absorbqkvo_pa_t_kernel(
                     start=True,
                     stop=True,
                 )
-            eng = "v" if (j, g) in S1_ON_VECTOR else "s"
             evac(eng, gv[:, g], bank[:].rearrange("p (t r) -> p r t", t=4))
 
         def q_ql(s):
@@ -242,27 +243,25 @@ def tile_absorbqkvo_pa_t_kernel(
             qls[s] = qlcp.tile([P, 256], U8, name="qls", tag="qls", align_bytes=64)
             nc.vector.quantize_mx(out=qlc[s][:].bitcast(FP8X4), scales=qls[s][:], in_=qlg[s][:])
 
-        cur = {}
+        outs = {}
+        pst = {}
 
-        def out_pair(q):
-            o0 = 2 * q
-            c = o0 // 4
-            j0 = o0 % 4
-            js = slice(j0, j0 + 2)
-            tail = q >= PAIRS - 1
-            bb = c // 2
-            rows = slice(512 * (c % 2), 512 * (c % 2) + 512)
-            if j0 == 0:
-                cur["qn"] = outp.tile([P, 2, 4, 256], F32, name="qn", tag="qn")
-                cur["kvn"] = outp.tile([P, 4, 256], F32, name="kvn", tag="kvn")
-                cur["rope"] = outp.tile([P, 3, 4, 64], F32, name="rope", tag="rope")
-                cur["v"] = outp.tile([P, 4, 64], F32, name="v_sb", tag="v_sb")
-            qn = cur["qn"]
-            kvn = cur["kvn"]
-            rope = cur["rope"]
-            v_sb = cur["v"]
+        def o_begin(q):
+            c = q // 2
+            if q % 2 == 0:
+                outs[c] = (
+                    outp.tile([P, 2, 4, 256], F32, name="qn", tag="qn"),
+                    outp.tile([P, 4, 256], F32, name="kvn", tag="kvn"),
+                    outp.tile([P, 3, 4, 64], F32, name="rope", tag="rope"),
+                    outp.tile([P, 4, 64], F32, name="v_sb", tag="v_sb"),
+                )
+
+        def o_kv(q, eng):
+            c = q // 2
+            j0 = 2 * (q % 2)
             r_b = psum.tile([P, 2, 256], F32, name="bank", tag="bank")
             kvn_b = psum.tile([P, 2, 256], F32, name="bank", tag="bank")
+            pst[q] = [r_b, None, None]
             for jj in range(2):
                 tok = slice((j0 + jj) * P, (j0 + jj + 1) * P)
                 nc.tensor.matmul_mx(
@@ -277,9 +276,12 @@ def tile_absorbqkvo_pa_t_kernel(
                     rhs=wkvc[:, 128:384].bitcast(FP8X4), rhs_scale=wkvs[:, 128:384],
                     start=True, stop=True,
                 )
-            evac("s", kvn[:, js, :], kvn_b[:])
+            evac(eng, outs[c][1][:, j0 : j0 + 2, :], kvn_b[:])
+
+        def o_qr(q):
+            r_b = pst[q][0]
             for jj in range(2):
-                o = o0 + jj
+                o = 2 * q + jj
                 for g in range(2):
                     nc.tensor.matmul_mx(
                         out=r_b[:, jj, 0:128],
@@ -289,92 +291,386 @@ def tile_absorbqkvo_pa_t_kernel(
                         rhs_scale=wqrs[:, P * g : P * (g + 1)],
                         start=(g == 0), stop=(g == 1),
                     )
+
+        def o_rope(q):
+            c = q // 2
+            j0 = 2 * (q % 2)
+            o0 = 2 * q
+            r_b = pst[q][0]
             x = r_b[:, :, 0:192].rearrange("p j (g f) -> p j g f", g=3)
             t1 = tmpp.tile([P, 2, 3, 64], F32, name="t1", tag="t1")
             t2 = tmpp.tile([P, 2, 3, 64], F32, name="t2", tag="t2")
+            pst[q][1] = t1
+            pst[q][2] = t2
             cv = cos_sb[:, o0 : o0 + 2, :].unsqueeze(2).to_broadcast([P, 2, 3, 64])
             sv = ssw_sb[:, o0 : o0 + 2, :].unsqueeze(2).to_broadcast([P, 2, 3, 64])
             nc.vector.tensor_tensor(out=t1[:], in0=x, in1=cv, op=MULT)
             nc.vector.tensor_tensor(out=t2[:], in0=x, in1=sv, op=MULT)
-            nc.vector.tensor_copy(out=v_sb[:, js, :], in_=r_b[:, :, 192:256])
-            add_eng = nc.gpsimd if (GADD and not tail) else nc.vector
+            nc.vector.tensor_copy(out=outs[c][3][:, j0 : j0 + 2, :], in_=r_b[:, :, 192:256])
+
+        def o_add(q):
+            c = q // 2
+            j0 = 2 * (q % 2)
+            t1 = pst[q][1]
+            t2 = pst[q][2]
+            add_eng = nc.gpsimd if (GADD and q < PAIRS - 1) else nc.vector
             for half in range(2):
                 a = slice(32 * half, 32 * half + 32)
                 b = slice(32 * (1 - half), 32 * (1 - half) + 32)
                 add_eng.tensor_tensor(
-                    out=rope[:, :, js, a],
+                    out=outs[c][2][:, :, j0 : j0 + 2, a],
                     in0=t1[:, :, :, a].rearrange("p j g i -> p g j i"),
                     in1=t2[:, :, :, b].rearrange("p j g i -> p g j i"),
                     op=ADD,
                 )
-            qdst = out_1[bb, :, rows, :].rearrange("h (p j) f -> p h j f", j=4)
-            for jj in range(2):
-                o = o0 + jj
-                j = j0 + jj
-                q_b = new_bank()
-                for g in range(2):
-                    nc.tensor.matmul_mx(
-                        out=q_b[:],
-                        lhsT=qlc[o][:, g * P : (g + 1) * P].bitcast(FP8X4),
-                        lhsT_scale=qls[o][:, g * P : (g + 1) * P],
-                        rhs=wqbc[:, 512 * g : 512 * (g + 1)].bitcast(FP8X4),
-                        rhs_scale=wqbs[:, 512 * g : 512 * (g + 1)],
-                        start=(g == 0), stop=(g == 1),
-                    )
-                evac("v" if (tail and jj == 0) else "s", qn[:, :, j, :], q_b[:].rearrange("p (h f) -> p h f", h=2))
-                if tail:
-                    nc.sync.dma_start(out=qdst[:, :, j : j + 1, :], in_=qn[:, :, j : j + 1, :])
-            fine = c == CHUNKS - 1
-            if fine or j0 == 2:
-                sl = js if fine else slice(0, 4)
-                if not tail:
-                    nc.sync.dma_start(out=qdst[:, :, sl, :], in_=qn[:, :, sl, :])
-                nc.sync.dma_start(
-                    out=out_4[bb, rows, :].rearrange("(p j) f -> p j f", j=4)[:, sl, :], in_=kvn[:, sl, :]
-                )
-                nc.sync.dma_start(
-                    out=out_3[bb, rows, :].rearrange("(p j) f -> p j f", j=4)[:, sl, :], in_=v_sb[:, sl, :]
-                )
-                nc.sync.dma_start(
-                    out=out_0[bb, :, rows, :].rearrange("h (p j) f -> p h j f", j=4)[:, :, sl, :],
-                    in_=rope[:, 0:2, sl, :],
-                )
-                nc.sync.dma_start(
-                    out=out_2[bb, rows, :].rearrange("(p j) f -> p j f", j=4)[:, sl, :], in_=rope[:, 2, sl, :]
-                )
 
-        tr_h(0)
-        prep_wqa(0)
+        def o_qn(q, jj, eng):
+            c = q // 2
+            j = 2 * (q % 2) + jj
+            o = 2 * q + jj
+            q_b = new_bank()
+            for g in range(2):
+                nc.tensor.matmul_mx(
+                    out=q_b[:],
+                    lhsT=qlc[o][:, g * P : (g + 1) * P].bitcast(FP8X4),
+                    lhsT_scale=qls[o][:, g * P : (g + 1) * P],
+                    rhs=wqbc[:, 512 * g : 512 * (g + 1)].bitcast(FP8X4),
+                    rhs_scale=wqbs[:, 512 * g : 512 * (g + 1)],
+                    start=(g == 0), stop=(g == 1),
+                )
+            evac(eng, outs[c][0][:, :, j, :], q_b[:].rearrange("p (h f) -> p h f", h=2))
+
+        def where(c):
+            return c // 2, slice(512 * (c % 2), 512 * (c % 2) + 512)
+
+        def st_qn(c, j0, nj):
+            bb, rows = where(c)
+            sl = slice(j0, j0 + nj)
+            nc.sync.dma_start(
+                out=out_1[bb, :, rows, :].rearrange("h (p j) f -> p h j f", j=4)[:, :, sl, :],
+                in_=outs[c][0][:, :, sl, :],
+            )
+
+        def st_kvn(c, j0, nj):
+            bb, rows = where(c)
+            sl = slice(j0, j0 + nj)
+            nc.sync.dma_start(
+                out=out_4[bb, rows, :].rearrange("(p j) f -> p j f", j=4)[:, sl, :], in_=outs[c][1][:, sl, :]
+            )
+
+        def st_small(c, j0, nj):
+            bb, rows = where(c)
+            sl = slice(j0, j0 + nj)
+            nc.sync.dma_start(
+                out=out_3[bb, rows, :].rearrange("(p j) f -> p j f", j=4)[:, sl, :], in_=outs[c][3][:, sl, :]
+            )
+            nc.sync.dma_start(
+                out=out_0[bb, :, rows, :].rearrange("h (p j) f -> p h j f", j=4)[:, :, sl, :],
+                in_=outs[c][2][:, 0:2, sl, :],
+            )
+            nc.sync.dma_start(
+                out=out_2[bb, rows, :].rearrange("(p j) f -> p j f", j=4)[:, sl, :], in_=outs[c][2][:, 2, sl, :]
+            )
+
+        loadh(0)
+        loadwqa(0)
+        loadwqa(1)
+        loadwqa(2)
+        loadwqa(3)
+        loadh(1)
+        loadwkv()
+        loadwqb()
+        loadh(2)
+        loadsin(0)
+        loadcos(0)
+        loadh(3)
+        loadsin(1)
+        loadcos(1)
+        loadh(4)
+        loadh(5)
+        loadh(6)
+        loadh(7)
+        swap(0)
+        swap(1)
+        tr_h(0, "v", "s")
+        prep_wqa(0, "s")
         q_h(0)
-        prep_wqa(1)
+        prep_wqa(1, "v")
         q_wqa(0)
-        prep_wqa(2)
+        prep_wqa(2, "s")
         q_wqa(1)
-        prep_wqa(3)
+        prep_wqa(3, "s")
         q_wqa(2)
         q_wqa(3)
-        for j in range(4):
-            s1_half(j, 0)
-        tr_h(1)
-        prep_wkv()
-        for j in range(4):
-            s1_half(j, 1)
-            q_ql(j)
-            if j == 0:
-                q_h(1)
-        prep_wqb()
-        q_wqb()
-        out_pair(0)
-        for q in range(2, PAIRS + 1):
-            if q % 2 == 0 and q // 2 + 1 < CHUNKS:
-                tr_h(q // 2 + 1)
-            if q < PAIRS:
-                for s in (2 * q, 2 * q + 1):
-                    s1_half(s, 0)
-                    s1_half(s, 1)
-            out_pair(q - 1)
-            if q % 2 == 0 and q // 2 + 1 < CHUNKS:
-                q_h(q // 2 + 1)
-            if q < PAIRS:
-                q_ql(2 * q)
-                q_ql(2 * q + 1)
+        s1_half(0, 0, "s")
+        s1_half(1, 0, "v")
+        s1_half(2, 0, "s")
+        s1_half(3, 0, "v")
+        tr_h(1, "s", "v")
+        prep_wkv("s", "s")
+        s1_half(0, 1, "v")
+        q_h(1)
+        s1_half(1, 1, "s")
+        q_ql(0)
+        s1_half(2, 1, "v")
+        q_ql(1)
+        s1_half(3, 1, "s")
+        q_ql(2)
+        q_ql(3)
+        s1_half(4, 0, "s")
+        s1_half(4, 1, "s")
+        s1_half(5, 0, "s")
+        s1_half(5, 1, "v")
+        prep_wqb(("s", "v", "s", "v", "s"))
+        tr_h(2, "s", "v")
+        q_ql(4)
+        q_ql(5)
+        q_h(2)
+        s1_half(6, 0, "s")
+        s1_half(6, 1, "v")
+        s1_half(7, 0, "s")
+        s1_half(7, 1, "v")
+        q_wkv()
+        q_wqr()
+        q_wqn()
+        q_ql(6)
+        q_ql(7)
+        tr_h(3, "v", "s")
+        s1_half(8, 0, "s")
+        s1_half(8, 1, "s")
+        s1_half(9, 0, "s")
+        s1_half(9, 1, "v")
+        q_ql(8)
+        q_ql(9)
+        o_begin(0)
+        o_kv(0, "s")
+        st_kvn(0, 0, 2)
+        o_qr(0)
+        o_rope(0)
+        o_add(0)
+        o_qn(0, 0, "s")
+        o_qn(0, 1, "s")
+        st_qn(0, 0, 2)
+        q_h(3)
+        s1_half(10, 0, "s")
+        s1_half(10, 1, "v")
+        s1_half(11, 0, "s")
+        s1_half(11, 1, "v")
+        q_ql(10)
+        q_ql(11)
+        o_begin(1)
+        o_kv(1, "s")
+        st_kvn(0, 2, 2)
+        o_qr(1)
+        o_rope(1)
+        o_add(1)
+        o_qn(1, 0, "s")
+        o_qn(1, 1, "s")
+        st_qn(0, 2, 2)
+        st_small(0, 0, 4)
+        o_begin(2)
+        o_kv(2, "s")
+        st_kvn(1, 0, 2)
+        o_qr(2)
+        o_rope(2)
+        o_add(2)
+        o_qn(2, 0, "s")
+        o_qn(2, 1, "s")
+        st_qn(1, 0, 2)
+        tr_h(4, "v", "s")
+        s1_half(12, 0, "s")
+        s1_half(12, 1, "s")
+        s1_half(13, 0, "s")
+        s1_half(13, 1, "v")
+        q_ql(12)
+        q_ql(13)
+        o_begin(3)
+        o_kv(3, "s")
+        st_kvn(1, 2, 2)
+        o_qr(3)
+        o_rope(3)
+        o_add(3)
+        o_qn(3, 0, "s")
+        o_qn(3, 1, "s")
+        st_qn(1, 2, 2)
+        st_small(1, 0, 4)
+        q_h(4)
+        s1_half(14, 0, "s")
+        s1_half(14, 1, "v")
+        s1_half(15, 0, "s")
+        s1_half(15, 1, "v")
+        q_ql(14)
+        q_ql(15)
+        o_begin(4)
+        o_kv(4, "s")
+        st_kvn(2, 0, 2)
+        o_qr(4)
+        o_rope(4)
+        o_add(4)
+        o_qn(4, 0, "s")
+        o_qn(4, 1, "s")
+        st_qn(2, 0, 2)
+        o_begin(5)
+        o_kv(5, "s")
+        st_kvn(2, 2, 2)
+        o_qr(5)
+        o_rope(5)
+        o_add(5)
+        o_qn(5, 0, "s")
+        o_qn(5, 1, "s")
+        st_qn(2, 2, 2)
+        st_small(2, 0, 4)
+        tr_h(5, "v", "s")
+        s1_half(16, 0, "s")
+        s1_half(16, 1, "s")
+        s1_half(17, 0, "s")
+        s1_half(17, 1, "v")
+        q_ql(16)
+        q_ql(17)
+        o_begin(6)
+        o_kv(6, "s")
+        st_kvn(3, 0, 2)
+        o_qr(6)
+        o_rope(6)
+        o_add(6)
+        o_qn(6, 0, "s")
+        o_qn(6, 1, "s")
+        st_qn(3, 0, 2)
+        q_h(5)
+        s1_half(18, 0, "s")
+        s1_half(18, 1, "v")
+        s1_half(19, 0, "s")
+        s1_half(19, 1, "v")
+        q_ql(18)
+        q_ql(19)
+        o_begin(7)
+        o_kv(7, "s")
+        st_kvn(3, 2, 2)
+        o_qr(7)
+        o_rope(7)
+        o_add(7)
+        o_qn(7, 0, "s")
+        o_qn(7, 1, "s")
+        st_qn(3, 2, 2)
+        st_small(3, 0, 4)
+        o_begin(8)
+        o_kv(8, "s")
+        st_kvn(4, 0, 2)
+        o_qr(8)
+        o_rope(8)
+        o_add(8)
+        o_qn(8, 0, "s")
+        o_qn(8, 1, "s")
+        st_qn(4, 0, 2)
+        tr_h(6, "v", "s")
+        s1_half(20, 0, "s")
+        s1_half(20, 1, "s")
+        s1_half(21, 0, "s")
+        s1_half(21, 1, "v")
+        q_ql(20)
+        q_ql(21)
+        o_begin(9)
+        o_kv(9, "s")
+        st_kvn(4, 2, 2)
+        o_qr(9)
+        o_rope(9)
+        o_add(9)
+        o_qn(9, 0, "s")
+        o_qn(9, 1, "s")
+        st_qn(4, 2, 2)
+        st_small(4, 0, 4)
+        q_h(6)
+        s1_half(22, 0, "s")
+        s1_half(22, 1, "v")
+        s1_half(23, 0, "s")
+        s1_half(23, 1, "v")
+        q_ql(22)
+        q_ql(23)
+        o_begin(10)
+        o_kv(10, "s")
+        st_kvn(5, 0, 2)
+        o_qr(10)
+        o_rope(10)
+        o_add(10)
+        o_qn(10, 0, "s")
+        o_qn(10, 1, "s")
+        st_qn(5, 0, 2)
+        tr_h(7, "v", "s")
+        s1_half(24, 0, "s")
+        s1_half(24, 1, "s")
+        s1_half(25, 0, "s")
+        s1_half(25, 1, "v")
+        q_ql(24)
+        q_ql(25)
+        o_begin(11)
+        o_kv(11, "s")
+        st_kvn(5, 2, 2)
+        o_qr(11)
+        o_rope(11)
+        o_add(11)
+        o_qn(11, 0, "s")
+        o_qn(11, 1, "s")
+        st_qn(5, 2, 2)
+        st_small(5, 0, 4)
+        q_h(7)
+        s1_half(26, 0, "s")
+        s1_half(26, 1, "v")
+        s1_half(27, 0, "s")
+        s1_half(27, 1, "v")
+        q_ql(26)
+        q_ql(27)
+        o_begin(12)
+        o_kv(12, "s")
+        st_kvn(6, 0, 2)
+        o_qr(12)
+        o_rope(12)
+        o_add(12)
+        o_qn(12, 0, "s")
+        st_qn(6, 0, 1)
+        o_qn(12, 1, "s")
+        st_qn(6, 1, 1)
+        s1_half(28, 0, "s")
+        s1_half(28, 1, "s")
+        s1_half(29, 0, "s")
+        s1_half(29, 1, "v")
+        q_ql(28)
+        q_ql(29)
+        o_begin(13)
+        o_kv(13, "s")
+        st_kvn(6, 2, 2)
+        o_qr(13)
+        o_rope(13)
+        o_add(13)
+        o_qn(13, 0, "s")
+        st_qn(6, 2, 1)
+        o_qn(13, 1, "s")
+        st_qn(6, 3, 1)
+        st_small(6, 0, 4)
+        s1_half(30, 0, "s")
+        s1_half(30, 1, "v")
+        s1_half(31, 0, "s")
+        s1_half(31, 1, "v")
+        q_ql(30)
+        q_ql(31)
+        o_begin(14)
+        o_kv(14, "s")
+        st_kvn(7, 0, 2)
+        o_qr(14)
+        o_rope(14)
+        o_add(14)
+        o_qn(14, 0, "s")
+        st_qn(7, 0, 1)
+        o_qn(14, 1, "s")
+        st_qn(7, 1, 1)
+        st_small(7, 0, 2)
+        o_begin(15)
+        o_kv(15, "s")
+        st_kvn(7, 2, 2)
+        o_qr(15)
+        o_rope(15)
+        o_add(15)
+        st_small(7, 2, 2)
+        o_qn(15, 0, "s")
+        st_qn(7, 2, 1)
+        o_qn(15, 1, "s")
+        st_qn(7, 3, 1)

@@ -12,665 +12,355 @@ MULT = mybir.AluOpType.mult
 ADD = mybir.AluOpType.add
 
 P = 128
+BANK = 512
 TOKENS = 4096
 HID = 512
 QLR = 1024
-STEPS = 32
-PAIRS = 16
-CHUNKS = 8
-PIN = True
-GADD = True
-FLOPS = 2 * TOKENS * (HID * QLR + QLR * 640 + HID * 384)
+ROT = 64
+NOPE = 256
+HEAD = ROT + NOPE
+CHUNKS = TOKENS // 512
+PAIRS = 2 * CHUNKS
+TILES = 4 * CHUNKS
+START_PAIRS = 4
+FLOPS = 2 * TOKENS * (HID * QLR + QLR * 2 * HEAD + HID * (2 * ROT + NOPE))
 
 
 def tile_absorbqkvo_pa_t_kernel(
     tc, hidden_states, cos, sin, w_qa, w_qb, w_kv, out_0, out_1, out_2, out_3, out_4
 ):
     nc = tc.nc
-    hflat = hidden_states.flatten_outer_dims()
-    cosf = cos.flatten_outer_dims()
-    sinf = sin.flatten_outer_dims()
+    h_rows = hidden_states.flatten_outer_dims()
+    cos_rows = cos.flatten_outer_dims()
+    sin_rows = sin.flatten_outer_dims()
+    scalar_copy = nc.scalar.copy
+    vector_copy = nc.vector.tensor_copy
 
     with ExitStack() as ctx:
-        if PIN:
-            ctx.enter_context(tc.manual_schedule())
+        ctx.enter_context(tc.manual_schedule())
         const = ctx.enter_context(tc.tile_pool(name="const", bufs=1))
-        hpool = ctx.enter_context(tc.tile_pool(name="hpool", bufs=CHUNKS))
-        hgp = ctx.enter_context(tc.tile_pool(name="hgp", bufs=2))
-        hcp = ctx.enter_context(tc.tile_pool(name="hcp", bufs=5))
-        qlgp = ctx.enter_context(tc.tile_pool(name="qlgp", bufs=6))
-        qlcp = ctx.enter_context(tc.tile_pool(name="qlcp", bufs=14))
-        outp = ctx.enter_context(tc.tile_pool(name="outp", bufs=3))
-        tmpp = ctx.enter_context(tc.tile_pool(name="tmpp", bufs=3))
+        h_pool = ctx.enter_context(tc.tile_pool(name="h_pool", bufs=CHUNKS))
+        grouped_pool = ctx.enter_context(tc.tile_pool(name="grouped_pool", bufs=2))
+        h_code_pool = ctx.enter_context(tc.tile_pool(name="h_code_pool", bufs=4))
+        ql_pool = ctx.enter_context(tc.tile_pool(name="ql_pool", bufs=6))
+        ql_code_pool = ctx.enter_context(tc.tile_pool(name="ql_code_pool", bufs=2 * START_PAIRS + 4))
+        out_pool = ctx.enter_context(tc.tile_pool(name="out_pool", bufs=3))
+        prod_pool = ctx.enter_context(tc.tile_pool(name="prod_pool", bufs=3))
         psum = ctx.enter_context(tc.psum_pool(name="psum", bufs=8))
 
-        def evac(eng, out, in_):
-            if eng == "s":
-                nc.scalar.copy(out=out, in_=in_)
-            else:
-                nc.vector.tensor_copy(out=out, in_=in_)
-
         def new_bank():
-            bank = psum.tile([P, 512], F32, name="bank", tag="bank")
+            bank = psum.tile([P, BANK], F32, name="bank", tag="bank")
             return bank
 
-        ident = const.tile([P, P], F32, name="ident", tag="ident")
-        make_identity(nc, ident[:])
+        identity = const.tile([P, P], F32, name="identity", tag="identity")
+        make_identity(nc, identity[:])
 
-        h_sb = []
-        for c in range(CHUNKS):
-            h_sb.append(hpool.tile([P, 2048], BF16, name="h_sb", tag="h_sb"))
+        h_sb = [h_pool.tile([P, 4 * HID], BF16, name="h_sb", tag="h_sb") for c in range(CHUNKS)]
+        wqa_sb = const.tile([P, 8 * HID], BF16, name="wqa_sb", tag="wqa_sb")
+        wkv_sb = const.tile([P, 3 * HID], BF16, name="wkv_sb", tag="wkv_sb")
+        wqb_sb = const.tile([P, 5 * QLR], BF16, name="wqb_sb", tag="wqb_sb")
+        cos_sb = const.tile([P, TILES, ROT], BF16, name="cos_sb", tag="cos_sb")
+        sin_sb = const.tile([P, TILES, ROT], BF16, name="sin_sb", tag="sin_sb")
+        partner_sin = const.tile([P, TILES, ROT], BF16, name="partner_sin", tag="partner_sin")
 
-        def loadh(c):
+        def load_h(c):
             nc.sync.dma_start(
                 out=h_sb[c][:],
-                in_=hflat[512 * c : 512 * (c + 1), :].rearrange("(p j) k -> p (j k)", j=4),
+                in_=h_rows[512 * c : 512 * (c + 1), :].rearrange("(p j) k -> p (j k)", j=4),
             )
 
-        wqa_sb = const.tile([P, 4096], BF16, name="wqa_sb", tag="wqa_sb")
-        wkv_sb = const.tile([P, 1536], BF16, name="wkv_sb", tag="wkv_sb")
-        wqb_sb = const.tile([P, 5120], BF16, name="wqb_sb", tag="wqb_sb")
-        cos_sb = const.tile([P, STEPS, 64], BF16, name="cos_sb", tag="cos_sb")
-        sin_sb = const.tile([P, STEPS, 64], BF16, name="sin_sb", tag="sin_sb")
-        ssw_sb = const.tile([P, STEPS, 64], BF16, name="ssw_sb", tag="ssw_sb")
-
-        def load_table(dst, src, part):
+        def load_table(table, rows, half):
             nc.sync.dma_start(
-                out=dst[:, 16 * part : 16 * (part + 1), :].rearrange("p (c j) f -> p c (j f)", j=4),
-                in_=src[2048 * part : 2048 * (part + 1), :].rearrange("(c p j) f -> p c (j f)", c=4, p=P, j=4),
+                out=table[:, 16 * half : 16 * (half + 1), :].rearrange("p (c j) f -> p c (j f)", j=4),
+                in_=rows[2048 * half : 2048 * (half + 1), :].rearrange("(c p j) f -> p c (j f)", c=4, p=P, j=4),
             )
 
-        def loadsin(part):
-            load_table(sin_sb, sinf, part)
+        wqa_rows = w_qa.rearrange("(m r e) k -> r m (e k)", m=4, r=P, e=2)
+        wqa_parts = wqa_sb[:].rearrange("p (m x) -> p m x", m=4)
 
-        def loadcos(part):
-            load_table(cos_sb, cosf, part)
+        load_h(0)
+        for m in range(4):
+            nc.sync.dma_start(out=wqa_parts[:, m, :], in_=wqa_rows[:, m, :])
+        load_h(1)
+        nc.sync.dma_start(
+            out=wkv_sb[:].rearrange("p (a k) -> p a k", a=3), in_=w_kv.rearrange("(a r) k -> r a k", a=3)
+        )
+        nc.sync.dma_start(
+            out=wqb_sb[:].rearrange("p (a k) -> p a k", a=5), in_=w_qb.rearrange("(a r) k -> r a k", a=5)
+        )
+        load_h(2)
+        load_table(sin_sb, sin_rows, 0)
+        load_table(cos_sb, cos_rows, 0)
+        load_h(3)
+        load_table(sin_sb, sin_rows, 1)
+        load_table(cos_sb, cos_rows, 1)
+        for c in range(4, CHUNKS):
+            load_h(c)
 
-        def swap(part):
-            st = slice(16 * part, 16 * (part + 1))
+        for half in range(2):
+            tiles = slice(16 * half, 16 * (half + 1))
             nc.gpsimd.tensor_scalar(
-                out=ssw_sb[:, st, 0:32], in0=sin_sb[:, st, 32:64], scalar1=1.0, scalar2=0.0, op0=MULT, op1=ADD
+                out=partner_sin[:, tiles, 0:32], in0=sin_sb[:, tiles, 32:64],
+                scalar1=1.0, scalar2=0.0, op0=MULT, op1=ADD,
             )
             nc.gpsimd.tensor_scalar(
-                out=ssw_sb[:, st, 32:64], in0=sin_sb[:, st, 0:32], scalar1=-1.0, scalar2=0.0, op0=MULT, op1=ADD
+                out=partner_sin[:, tiles, 32:64], in0=sin_sb[:, tiles, 0:32],
+                scalar1=-1.0, scalar2=0.0, op0=MULT, op1=ADD,
             )
 
-        wqa_src = w_qa.rearrange("(m r e) k -> r m (e k)", m=4, r=P, e=2)
-        wqa_dst = wqa_sb[:].rearrange("p (m x) -> p m x", m=4)
-
-        def loadwqa(m):
-            nc.sync.dma_start(out=wqa_dst[:, m, :], in_=wqa_src[:, m, :])
-
-        def loadwkv():
-            nc.sync.dma_start(
-                out=wkv_sb[:].rearrange("p (a k) -> p a k", a=3),
-                in_=w_kv.rearrange("(a r) k -> r a k", a=3),
-            )
-
-        def loadwqb():
-            nc.sync.dma_start(
-                out=wqb_sb[:].rearrange("p (a k) -> p a k", a=5),
-                in_=w_qb.rearrange("(a r) k -> r a k", a=5),
-            )
-
-        def transposes(src_words, offsets):
+        def transposed(words, starts):
             bank = new_bank()
-            for i, off in enumerate(offsets):
-                nc.tensor.transpose(bank[:, i * P : (i + 1) * P], src_words[:, off : off + P], ident[:])
+            for i, start in enumerate(starts):
+                nc.tensor.transpose(bank[:, i * P : (i + 1) * P], words[:, start : start + P], identity[:])
             return bank
 
-        def transpose_block(src_words, offsets, dst, eng):
-            n = len(offsets) // 2
-            bank = transposes(src_words, offsets)
-            evac(eng, dst, bank[:, 0 : n * 256].rearrange("p (a u r) -> p a r u", a=n, u=2))
+        def row_blocks(first, count, words_per_row):
+            return [words_per_row * (first + a) + P * u for a in range(count) for u in range(2)]
 
-        hc = {}
-        hs = {}
-        hg = {}
+        def word_view(grouped, blocks):
+            return grouped[:].bitcast(F32).rearrange("p (a r u) -> p a r u", a=blocks, u=2)
 
-        def tr_h(c, e0, e1):
-            g = hgp.tile([P, 2048], BF16, name="hg", tag="hg", align_bytes=64)
-            hg[c] = g
-            gv = g[:].bitcast(F32).rearrange("p (j r u) -> p j r u", j=4, u=2)
-            words = h_sb[c][:].bitcast(F32)
+        def regroup(copy, dst, bank, blocks):
+            copy(out=dst, in_=bank[:, 0 : 2 * P * blocks].rearrange("p (a u r) -> p a r u", a=blocks, u=2))
+
+        def quantise(codes, scales, grouped):
+            nc.vector.quantize_mx(out=codes.bitcast(FP8X4), scales=scales, in_=grouped)
+
+        h_grouped = {}
+        h_codes = {}
+        h_scales = {}
+
+        def transpose_h(c, copies):
+            h_grouped[c] = grouped_pool.tile([P, 4 * BANK], BF16, name="h_grouped", tag="h_grouped", align_bytes=64)
+            dst = word_view(h_grouped[c], 4)
             for b in range(2):
-                offs = [256 * (2 * b + a) + P * u for a in range(2) for u in range(2)]
-                transpose_block(words, offs, gv[:, 2 * b : 2 * b + 2], e0 if b == 0 else e1)
+                bank = transposed(h_sb[c][:].bitcast(F32), row_blocks(2 * b, 2, HID // 2))
+                regroup(copies[b], dst[:, 2 * b : 2 * b + 2], bank, 2)
 
-        def q_h(c):
-            hc[c] = hcp.tile([P, 512], U32, name="hc", tag="hc", align_bytes=64)
-            hs[c] = hcp.tile([P, 512], U8, name="hs", tag="hs", align_bytes=64)
-            nc.vector.quantize_mx(out=hc[c][:].bitcast(FP8X4), scales=hs[c][:], in_=hg[c][:])
+        def quantise_h(c):
+            h_codes[c] = h_code_pool.tile([P, BANK], U32, name="h_codes", tag="h_codes", align_bytes=64)
+            h_scales[c] = h_code_pool.tile([P, BANK], U8, name="h_scales", tag="h_scales", align_bytes=64)
+            quantise(h_codes[c][:], h_scales[c][:], h_grouped[c][:])
 
-        wqag = const.tile([P, 4096], BF16, name="wqag", tag="wqag", align_bytes=64)
-        wqac = const.tile([P, 1024], U32, name="wqac", tag="wqac", align_bytes=64)
-        wqas = const.tile([P, 1024], U8, name="wqas", tag="wqas", align_bytes=64)
+        wqa_grouped = const.tile([P, 8 * BANK], BF16, name="wqa_grouped", tag="wqa_grouped", align_bytes=64)
+        wqa_codes = const.tile([P, 8 * P], U32, name="wqa_codes", tag="wqa_codes", align_bytes=64)
+        wqa_scales = const.tile([P, 8 * P], U8, name="wqa_scales", tag="wqa_scales", align_bytes=64)
 
-        def prep_wqa(m, eng):
-            gv = wqag[:].bitcast(F32).rearrange("p (m r u) -> p m r u", m=8, u=2)
-            words = wqa_sb[:].bitcast(F32)
-            offs = [256 * (2 * m + a) + P * u for a in range(2) for u in range(2)]
-            transpose_block(words, offs, gv[:, 2 * m : 2 * m + 2], eng)
+        def transpose_wqa(m, copy):
+            bank = transposed(wqa_sb[:].bitcast(F32), row_blocks(2 * m, 2, HID // 2))
+            regroup(copy, word_view(wqa_grouped, 8)[:, 2 * m : 2 * m + 2], bank, 2)
 
-        def q_wqa(m):
-            nc.vector.quantize_mx(
-                out=wqac[:, 256 * m : 256 * (m + 1)].bitcast(FP8X4),
-                scales=wqas[:, 256 * m : 256 * (m + 1)],
-                in_=wqag[:, 1024 * m : 1024 * (m + 1)],
-            )
+        def quantise_wqa(m):
+            cols = slice(2 * P * m, 2 * P * (m + 1))
+            quantise(wqa_codes[:, cols], wqa_scales[:, cols], wqa_grouped[:, 2 * BANK * m : 2 * BANK * (m + 1)])
 
-        wkvg = const.tile([P, 1536], BF16, name="wkvg", tag="wkvg", align_bytes=64)
-        wkvc = const.tile([P, 384], U32, name="wkvc", tag="wkvc", align_bytes=64)
-        wkvs = const.tile([P, 384], U8, name="wkvs", tag="wkvs", align_bytes=64)
+        wkv_grouped = const.tile([P, 3 * BANK], BF16, name="wkv_grouped", tag="wkv_grouped", align_bytes=64)
+        wkv_codes = const.tile([P, 3 * P], U32, name="wkv_codes", tag="wkv_codes", align_bytes=64)
+        wkv_scales = const.tile([P, 3 * P], U8, name="wkv_scales", tag="wkv_scales", align_bytes=64)
+        KV_ROT = slice(0, 2 * ROT)
+        KV_NOPE = slice(2 * ROT, 2 * ROT + NOPE)
 
-        def prep_wkv(e0, e1):
-            gv = wkvg[:].bitcast(F32).rearrange("p (a r u) -> p a r u", a=3, u=2)
+        def transpose_wkv():
+            dst = word_view(wkv_grouped, 3)
             words = wkv_sb[:].bitcast(F32)
-            transpose_block(words, [0, 128, 256, 384], gv[:, 0:2], e0)
-            transpose_block(words, [512, 640], gv[:, 2:3], e1)
+            regroup(scalar_copy, dst[:, 0:2], transposed(words, row_blocks(0, 2, HID // 2)), 2)
+            regroup(scalar_copy, dst[:, 2:3], transposed(words, row_blocks(2, 1, HID // 2)), 1)
 
-        def q_wkv():
-            nc.vector.quantize_mx(
-                out=wkvc[:, 0:128].bitcast(FP8X4), scales=wkvs[:, 0:128], in_=wkvg[:, 0:512]
-            )
-            nc.vector.quantize_mx(
-                out=wkvc[:, 128:384].bitcast(FP8X4), scales=wkvs[:, 128:384], in_=wkvg[:, 512:1536]
-            )
+        def quantise_wkv():
+            quantise(wkv_codes[:, KV_ROT], wkv_scales[:, KV_ROT], wkv_grouped[:, 0:BANK])
+            quantise(wkv_codes[:, KV_NOPE], wkv_scales[:, KV_NOPE], wkv_grouped[:, BANK : 3 * BANK])
 
-        wqbg = const.tile([P, 4096], BF16, name="wqbg", tag="wqbg", align_bytes=64)
-        wqbc = const.tile([P, 1024], U32, name="wqbc", tag="wqbc", align_bytes=64)
-        wqbs = const.tile([P, 1024], U8, name="wqbs", tag="wqbs", align_bytes=64)
-        wqrg = const.tile([P, 1024], BF16, name="wqrg", tag="wqrg", align_bytes=64)
-        wqrc = const.tile([P, 256], U32, name="wqrc", tag="wqrc", align_bytes=64)
-        wqrs = const.tile([P, 256], U8, name="wqrs", tag="wqrs", align_bytes=64)
+        nope_grouped = const.tile([P, 8 * BANK], BF16, name="nope_grouped", tag="nope_grouped", align_bytes=64)
+        nope_codes = const.tile([P, 2 * BANK], U32, name="nope_codes", tag="nope_codes", align_bytes=64)
+        nope_scales = const.tile([P, 2 * BANK], U8, name="nope_scales", tag="nope_scales", align_bytes=64)
+        rot_grouped = const.tile([P, 2 * BANK], BF16, name="rot_grouped", tag="rot_grouped", align_bytes=64)
+        rot_codes = const.tile([P, 2 * P], U32, name="rot_codes", tag="rot_codes", align_bytes=64)
+        rot_scales = const.tile([P, 2 * P], U8, name="rot_scales", tag="rot_scales", align_bytes=64)
 
-        WQB_RUNS = (
-            ((0, 64, True, 0), (64, 64, False, 0)),
-            ((0, 128, False, 64),),
-            ((0, 64, False, 192), (64, 64, True, 64)),
-            ((0, 128, False, 256),),
-            ((0, 128, False, 384),),
-        )
-
-        def prep_wqb(engs):
-            gv = wqbg[:].bitcast(F32).rearrange("p (g n u) -> p g n u", g=2, u=2)
-            rv = wqrg[:].bitcast(F32).rearrange("p (g n u) -> p g n u", g=2, u=2)
+        def transpose_wqb():
+            nope_dst = nope_grouped[:].bitcast(F32).rearrange("p (g n u) -> p g n u", g=2, u=2)
+            rot_dst = rot_grouped[:].bitcast(F32).rearrange("p (g n u) -> p g n u", g=2, u=2)
             words = wqb_sb[:].bitcast(F32)
             for a in range(5):
-                offs = [512 * a + 256 * g + P * u for g in range(2) for u in range(2)]
-                bank = transposes(words, offs)
-                bv = bank[:].rearrange("p (g u r) -> p g r u", g=2, u=2)
-                for r0, nr, rotary, n0 in WQB_RUNS[a]:
-                    dst = rv if rotary else gv
-                    evac(engs[a], dst[:, :, n0 : n0 + nr, :], bv[:, :, r0 : r0 + nr, :])
+                bank = transposed(words, [QLR // 2 * a + 2 * P * g + P * u for g in range(2) for u in range(2)])
+                src = bank[:].rearrange("p (g u r) -> p g r u", g=2, u=2)
+                copy = vector_copy if a % 2 else scalar_copy
+                for head in range(2):
+                    for first, count, dst, col in (
+                        (HEAD * head, ROT, rot_dst, ROT * head),
+                        (HEAD * head + ROT, NOPE, nope_dst, NOPE * head),
+                    ):
+                        lo = max(first, P * a)
+                        hi = min(first + count, P * (a + 1))
+                        if lo < hi:
+                            copy(
+                                out=dst[:, :, col + lo - first : col + hi - first, :],
+                                in_=src[:, :, lo - P * a : hi - P * a, :],
+                            )
 
-        def q_wqr():
-            nc.vector.quantize_mx(out=wqrc[:].bitcast(FP8X4), scales=wqrs[:], in_=wqrg[:])
-
-        def q_wqn():
+        def quantise_wqb():
+            quantise(rot_codes[:], rot_scales[:], rot_grouped[:])
             for g in range(2):
-                nc.vector.quantize_mx(
-                    out=wqbc[:, 512 * g : 512 * (g + 1)].bitcast(FP8X4),
-                    scales=wqbs[:, 512 * g : 512 * (g + 1)],
-                    in_=wqbg[:, 2048 * g : 2048 * (g + 1)],
-                )
+                cols = slice(BANK * g, BANK * (g + 1))
+                quantise(nope_codes[:, cols], nope_scales[:, cols], nope_grouped[:, 4 * BANK * g : 4 * BANK * (g + 1)])
 
-        qlg = {}
-        qlc = {}
-        qls = {}
+        ql_grouped = {}
+        ql_codes = {}
+        ql_scales = {}
 
-        def s1_half(s, g, eng):
+        def q_lora_bank(s, g, copy):
             c, j = divmod(s, 4)
-            if s not in qlg:
-                qlg[s] = qlgp.tile([P, 1024], BF16, name="qlg", tag="qlg", align_bytes=64)
-            gv = qlg[s][:].rearrange("p (g r t) -> p g r t", g=2, t=4)
+            if g == 0:
+                ql_grouped[s] = ql_pool.tile([P, 2 * BANK], BF16, name="ql_grouped", tag="ql_grouped", align_bytes=64)
+            tok = slice(P * j, P * (j + 1))
             bank = new_bank()
             for t in range(4):
-                m = 4 * g + t
+                feat = slice(P * (4 * g + t), P * (4 * g + t + 1))
                 nc.tensor.matmul_mx(
-                    out=bank[:, t * P : (t + 1) * P],
-                    lhsT=wqac[:, m * P : (m + 1) * P].bitcast(FP8X4),
-                    lhsT_scale=wqas[:, m * P : (m + 1) * P],
-                    rhs=hc[c][:, j * P : (j + 1) * P].bitcast(FP8X4),
-                    rhs_scale=hs[c][:, j * P : (j + 1) * P],
-                    start=True,
-                    stop=True,
-                )
-            evac(eng, gv[:, g], bank[:].rearrange("p (t r) -> p r t", t=4))
-
-        def q_ql(s):
-            qlc[s] = qlcp.tile([P, 256], U32, name="qlc", tag="qlc", align_bytes=64)
-            qls[s] = qlcp.tile([P, 256], U8, name="qls", tag="qls", align_bytes=64)
-            nc.vector.quantize_mx(out=qlc[s][:].bitcast(FP8X4), scales=qls[s][:], in_=qlg[s][:])
-
-        outs = {}
-        pst = {}
-
-        def o_begin(q):
-            c = q // 2
-            if q % 2 == 0:
-                outs[c] = (
-                    outp.tile([P, 2, 4, 256], F32, name="qn", tag="qn"),
-                    outp.tile([P, 4, 256], F32, name="kvn", tag="kvn"),
-                    outp.tile([P, 3, 4, 64], F32, name="rope", tag="rope"),
-                    outp.tile([P, 4, 64], F32, name="v_sb", tag="v_sb"),
-                )
-
-        def o_kv(q, eng):
-            c = q // 2
-            j0 = 2 * (q % 2)
-            r_b = psum.tile([P, 2, 256], F32, name="bank", tag="bank")
-            kvn_b = psum.tile([P, 2, 256], F32, name="bank", tag="bank")
-            pst[q] = [r_b, None, None]
-            for jj in range(2):
-                tok = slice((j0 + jj) * P, (j0 + jj + 1) * P)
-                nc.tensor.matmul_mx(
-                    out=r_b[:, jj, 128:256],
-                    lhsT=hc[c][:, tok].bitcast(FP8X4), lhsT_scale=hs[c][:, tok],
-                    rhs=wkvc[:, 0:128].bitcast(FP8X4), rhs_scale=wkvs[:, 0:128],
+                    out=bank[:, P * t : P * (t + 1)],
+                    lhsT=wqa_codes[:, feat].bitcast(FP8X4), lhsT_scale=wqa_scales[:, feat],
+                    rhs=h_codes[c][:, tok].bitcast(FP8X4), rhs_scale=h_scales[c][:, tok],
                     start=True, stop=True,
                 )
-                nc.tensor.matmul_mx(
-                    out=kvn_b[:, jj, :],
-                    lhsT=hc[c][:, tok].bitcast(FP8X4), lhsT_scale=hs[c][:, tok],
-                    rhs=wkvc[:, 128:384].bitcast(FP8X4), rhs_scale=wkvs[:, 128:384],
-                    start=True, stop=True,
-                )
-            evac(eng, outs[c][1][:, j0 : j0 + 2, :], kvn_b[:])
+            copy(
+                out=ql_grouped[s][:, BANK * g : BANK * (g + 1)].rearrange("p (r t) -> p r t", t=4),
+                in_=bank[:].rearrange("p (t r) -> p r t", t=4),
+            )
 
-        def o_qr(q):
-            r_b = pst[q][0]
-            for jj in range(2):
-                o = 2 * q + jj
-                for g in range(2):
+        def q_lora_pair(q):
+            for s in (2 * q, 2 * q + 1):
+                q_lora_bank(s, 0, scalar_copy)
+                q_lora_bank(s, 1, vector_copy)
+
+        def quantise_q_lora(s):
+            ql_codes[s] = ql_code_pool.tile([P, 2 * P], U32, name="ql_codes", tag="ql_codes", align_bytes=64)
+            ql_scales[s] = ql_code_pool.tile([P, 2 * P], U8, name="ql_scales", tag="ql_scales", align_bytes=64)
+            quantise(ql_codes[s][:], ql_scales[s][:], ql_grouped[s][:])
+
+        chunk_out = {}
+
+        def q_passes(out, s, codes, scales, width):
+            for g in range(2):
+                tok = slice(P * g, P * (g + 1))
+                cols = slice(width * g, width * (g + 1))
+                nc.tensor.matmul_mx(
+                    out=out,
+                    lhsT=ql_codes[s][:, tok].bitcast(FP8X4), lhsT_scale=ql_scales[s][:, tok],
+                    rhs=codes[:, cols].bitcast(FP8X4), rhs_scale=scales[:, cols],
+                    start=(g == 0), stop=(g == 1),
+                )
+
+        def output_pair(q):
+            c, second = divmod(q, 2)
+            j0 = 2 * second
+            pair = slice(j0, j0 + 2)
+            last_chunk = c == CHUNKS - 1
+            if not second:
+                chunk_out[c] = (
+                    out_pool.tile([P, 2, 4, NOPE], F32, name="q_nope", tag="q_nope"),
+                    out_pool.tile([P, 4, NOPE], F32, name="kv_nope", tag="kv_nope"),
+                    out_pool.tile([P, 3, 4, ROT], F32, name="rotated", tag="rotated"),
+                    out_pool.tile([P, 4, ROT], F32, name="v_rope", tag="v_rope"),
+                )
+            q_nope, kv_nope, rotated, v_rope = chunk_out[c]
+            batch = c // 2
+            rows = slice(512 * (c % 2), 512 * (c % 2) + 512)
+            q_nope_dram = out_1[batch, :, rows, :].rearrange("h (p j) f -> p h j f", j=4)
+            q_rope_dram = out_0[batch, :, rows, :].rearrange("h (p j) f -> p h j f", j=4)
+            k_rope_dram = out_2[batch, rows, :].rearrange("(p j) f -> p j f", j=4)
+            v_rope_dram = out_3[batch, rows, :].rearrange("(p j) f -> p j f", j=4)
+            kv_nope_dram = out_4[batch, rows, :].rearrange("(p j) f -> p j f", j=4)
+
+            small_bank = psum.tile([P, 2, 4 * ROT], F32, name="bank", tag="bank")
+            kv_nope_bank = psum.tile([P, 2, NOPE], F32, name="bank", tag="bank")
+            for i in range(2):
+                tok = slice(P * (j0 + i), P * (j0 + i + 1))
+                for out, cols in ((small_bank[:, i, 2 * ROT : 4 * ROT], KV_ROT), (kv_nope_bank[:, i, :], KV_NOPE)):
                     nc.tensor.matmul_mx(
-                        out=r_b[:, jj, 0:128],
-                        lhsT=qlc[o][:, g * P : (g + 1) * P].bitcast(FP8X4),
-                        lhsT_scale=qls[o][:, g * P : (g + 1) * P],
-                        rhs=wqrc[:, P * g : P * (g + 1)].bitcast(FP8X4),
-                        rhs_scale=wqrs[:, P * g : P * (g + 1)],
-                        start=(g == 0), stop=(g == 1),
+                        out=out,
+                        lhsT=h_codes[c][:, tok].bitcast(FP8X4), lhsT_scale=h_scales[c][:, tok],
+                        rhs=wkv_codes[:, cols].bitcast(FP8X4), rhs_scale=wkv_scales[:, cols],
+                        start=True, stop=True,
                     )
+            scalar_copy(out=kv_nope[:, pair, :], in_=kv_nope_bank[:])
+            nc.sync.dma_start(out=kv_nope_dram[:, pair, :], in_=kv_nope[:, pair, :])
+            for i in range(2):
+                q_passes(small_bank[:, i, 0 : 2 * ROT], 2 * q + i, rot_codes, rot_scales, 2 * ROT)
 
-        def o_rope(q):
-            c = q // 2
-            j0 = 2 * (q % 2)
-            o0 = 2 * q
-            r_b = pst[q][0]
-            x = r_b[:, :, 0:192].rearrange("p j (g f) -> p j g f", g=3)
-            t1 = tmpp.tile([P, 2, 3, 64], F32, name="t1", tag="t1")
-            t2 = tmpp.tile([P, 2, 3, 64], F32, name="t2", tag="t2")
-            pst[q][1] = t1
-            pst[q][2] = t2
-            cv = cos_sb[:, o0 : o0 + 2, :].unsqueeze(2).to_broadcast([P, 2, 3, 64])
-            sv = ssw_sb[:, o0 : o0 + 2, :].unsqueeze(2).to_broadcast([P, 2, 3, 64])
-            nc.vector.tensor_tensor(out=t1[:], in0=x, in1=cv, op=MULT)
-            nc.vector.tensor_tensor(out=t2[:], in0=x, in1=sv, op=MULT)
-            nc.vector.tensor_copy(out=outs[c][3][:, j0 : j0 + 2, :], in_=r_b[:, :, 192:256])
-
-        def o_add(q):
-            c = q // 2
-            j0 = 2 * (q % 2)
-            t1 = pst[q][1]
-            t2 = pst[q][2]
-            add_eng = nc.gpsimd if (GADD and q < PAIRS - 1) else nc.vector
-            for half in range(2):
-                a = slice(32 * half, 32 * half + 32)
-                b = slice(32 * (1 - half), 32 * (1 - half) + 32)
-                add_eng.tensor_tensor(
-                    out=outs[c][2][:, :, j0 : j0 + 2, a],
-                    in0=t1[:, :, :, a].rearrange("p j g i -> p g j i"),
-                    in1=t2[:, :, :, b].rearrange("p j g i -> p g j i"),
+            x = small_bank[:, :, 0 : 3 * ROT].rearrange("p j (n f) -> p j n f", n=3)
+            by_cos = prod_pool.tile([P, 2, 3, ROT], F32, name="by_cos", tag="by_cos")
+            by_sin = prod_pool.tile([P, 2, 3, ROT], F32, name="by_sin", tag="by_sin")
+            for prod, table in ((by_cos, cos_sb), (by_sin, partner_sin)):
+                nc.vector.tensor_tensor(
+                    out=prod[:], in0=x, op=MULT,
+                    in1=table[:, 2 * q : 2 * q + 2, :].unsqueeze(2).to_broadcast([P, 2, 3, ROT]),
+                )
+            vector_copy(out=v_rope[:, pair, :], in_=small_bank[:, :, 3 * ROT : 4 * ROT])
+            adder = nc.vector if q == PAIRS - 1 else nc.gpsimd
+            for mine, partner in ((slice(0, 32), slice(32, 64)), (slice(32, 64), slice(0, 32))):
+                adder.tensor_tensor(
+                    out=rotated[:, :, pair, mine],
+                    in0=by_cos[:, :, :, mine].rearrange("p j n f -> p n j f"),
+                    in1=by_sin[:, :, :, partner].rearrange("p j n f -> p n j f"),
                     op=ADD,
                 )
 
-        def o_qn(q, jj, eng):
-            c = q // 2
-            j = 2 * (q % 2) + jj
-            o = 2 * q + jj
-            q_b = new_bank()
-            for g in range(2):
-                nc.tensor.matmul_mx(
-                    out=q_b[:],
-                    lhsT=qlc[o][:, g * P : (g + 1) * P].bitcast(FP8X4),
-                    lhsT_scale=qls[o][:, g * P : (g + 1) * P],
-                    rhs=wqbc[:, 512 * g : 512 * (g + 1)].bitcast(FP8X4),
-                    rhs_scale=wqbs[:, 512 * g : 512 * (g + 1)],
-                    start=(g == 0), stop=(g == 1),
-                )
-            evac(eng, outs[c][0][:, :, j, :], q_b[:].rearrange("p (h f) -> p h f", h=2))
+            for i in range(2):
+                j = j0 + i
+                nope_bank = new_bank()
+                q_passes(nope_bank[:], 2 * q + i, nope_codes, nope_scales, BANK)
+                scalar_copy(out=q_nope[:, :, j, :], in_=nope_bank[:].rearrange("p (h f) -> p h f", h=2))
+                if last_chunk:
+                    nc.sync.dma_start(out=q_nope_dram[:, :, j : j + 1, :], in_=q_nope[:, :, j : j + 1, :])
+            if not last_chunk:
+                nc.sync.dma_start(out=q_nope_dram[:, :, pair, :], in_=q_nope[:, :, pair, :])
+            if last_chunk or second:
+                done = pair if last_chunk else slice(0, 4)
+                nc.sync.dma_start(out=v_rope_dram[:, done, :], in_=v_rope[:, done, :])
+                nc.sync.dma_start(out=q_rope_dram[:, :, done, :], in_=rotated[:, 0:2, done, :])
+                nc.sync.dma_start(out=k_rope_dram[:, done, :], in_=rotated[:, 2, done, :])
 
-        def where(c):
-            return c // 2, slice(512 * (c % 2), 512 * (c % 2) + 512)
+        transpose_h(0, (vector_copy, scalar_copy))
+        transpose_wqa(0, scalar_copy)
+        quantise_h(0)
+        for m in range(1, 4):
+            transpose_wqa(m, vector_copy if m % 2 else scalar_copy)
+            quantise_wqa(m - 1)
+        quantise_wqa(3)
+        for j in range(4):
+            q_lora_bank(j, 0, vector_copy if j % 2 else scalar_copy)
+        transpose_h(1, (vector_copy, scalar_copy))
+        transpose_wkv()
+        for j in range(4):
+            q_lora_bank(j, 1, scalar_copy if j % 2 else vector_copy)
+            if j == 0:
+                quantise_h(1)
+            else:
+                quantise_q_lora(j - 1)
+        quantise_q_lora(3)
+        q_lora_pair(2)
+        transpose_wqb()
+        transpose_h(2, (vector_copy, scalar_copy))
+        quantise_h(2)
+        quantise_wkv()
+        quantise_wqb()
+        q_lora_pair(3)
+        for s in range(4, 8):
+            quantise_q_lora(s)
 
-        def st_qn(c, j0, nj):
-            bb, rows = where(c)
-            sl = slice(j0, j0 + nj)
-            nc.sync.dma_start(
-                out=out_1[bb, :, rows, :].rearrange("h (p j) f -> p h j f", j=4)[:, :, sl, :],
-                in_=outs[c][0][:, :, sl, :],
-            )
-
-        def st_kvn(c, j0, nj):
-            bb, rows = where(c)
-            sl = slice(j0, j0 + nj)
-            nc.sync.dma_start(
-                out=out_4[bb, rows, :].rearrange("(p j) f -> p j f", j=4)[:, sl, :], in_=outs[c][1][:, sl, :]
-            )
-
-        def st_small(c, j0, nj):
-            bb, rows = where(c)
-            sl = slice(j0, j0 + nj)
-            nc.sync.dma_start(
-                out=out_3[bb, rows, :].rearrange("(p j) f -> p j f", j=4)[:, sl, :], in_=outs[c][3][:, sl, :]
-            )
-            nc.sync.dma_start(
-                out=out_0[bb, :, rows, :].rearrange("h (p j) f -> p h j f", j=4)[:, :, sl, :],
-                in_=outs[c][2][:, 0:2, sl, :],
-            )
-            nc.sync.dma_start(
-                out=out_2[bb, rows, :].rearrange("(p j) f -> p j f", j=4)[:, sl, :], in_=outs[c][2][:, 2, sl, :]
-            )
-
-        loadh(0)
-        loadwqa(0)
-        loadwqa(1)
-        loadwqa(2)
-        loadwqa(3)
-        loadh(1)
-        loadwkv()
-        loadwqb()
-        loadh(2)
-        loadsin(0)
-        loadcos(0)
-        loadh(3)
-        loadsin(1)
-        loadcos(1)
-        loadh(4)
-        loadh(5)
-        loadh(6)
-        loadh(7)
-        swap(0)
-        swap(1)
-        tr_h(0, "v", "s")
-        prep_wqa(0, "s")
-        q_h(0)
-        prep_wqa(1, "v")
-        q_wqa(0)
-        prep_wqa(2, "s")
-        q_wqa(1)
-        prep_wqa(3, "s")
-        q_wqa(2)
-        q_wqa(3)
-        s1_half(0, 0, "s")
-        s1_half(1, 0, "v")
-        s1_half(2, 0, "s")
-        s1_half(3, 0, "v")
-        tr_h(1, "s", "v")
-        prep_wkv("s", "s")
-        s1_half(0, 1, "v")
-        q_h(1)
-        s1_half(1, 1, "s")
-        q_ql(0)
-        s1_half(2, 1, "v")
-        q_ql(1)
-        s1_half(3, 1, "s")
-        q_ql(2)
-        q_ql(3)
-        s1_half(4, 0, "s")
-        s1_half(4, 1, "s")
-        s1_half(5, 0, "s")
-        s1_half(5, 1, "v")
-        prep_wqb(("s", "v", "s", "v", "s"))
-        tr_h(2, "s", "v")
-        q_ql(4)
-        q_ql(5)
-        q_h(2)
-        s1_half(6, 0, "s")
-        s1_half(6, 1, "v")
-        s1_half(7, 0, "s")
-        s1_half(7, 1, "v")
-        q_wkv()
-        q_wqr()
-        q_wqn()
-        q_ql(6)
-        q_ql(7)
-        tr_h(3, "v", "s")
-        s1_half(8, 0, "s")
-        s1_half(8, 1, "s")
-        s1_half(9, 0, "s")
-        s1_half(9, 1, "v")
-        q_ql(8)
-        q_ql(9)
-        o_begin(0)
-        o_kv(0, "s")
-        st_kvn(0, 0, 2)
-        o_qr(0)
-        o_rope(0)
-        o_add(0)
-        o_qn(0, 0, "s")
-        o_qn(0, 1, "s")
-        st_qn(0, 0, 2)
-        q_h(3)
-        s1_half(10, 0, "s")
-        s1_half(10, 1, "v")
-        s1_half(11, 0, "s")
-        s1_half(11, 1, "v")
-        q_ql(10)
-        q_ql(11)
-        o_begin(1)
-        o_kv(1, "s")
-        st_kvn(0, 2, 2)
-        o_qr(1)
-        o_rope(1)
-        o_add(1)
-        o_qn(1, 0, "s")
-        o_qn(1, 1, "s")
-        st_qn(0, 2, 2)
-        st_small(0, 0, 4)
-        o_begin(2)
-        o_kv(2, "s")
-        st_kvn(1, 0, 2)
-        o_qr(2)
-        o_rope(2)
-        o_add(2)
-        o_qn(2, 0, "s")
-        o_qn(2, 1, "s")
-        st_qn(1, 0, 2)
-        tr_h(4, "v", "s")
-        s1_half(12, 0, "s")
-        s1_half(12, 1, "s")
-        s1_half(13, 0, "s")
-        s1_half(13, 1, "v")
-        q_ql(12)
-        q_ql(13)
-        o_begin(3)
-        o_kv(3, "s")
-        st_kvn(1, 2, 2)
-        o_qr(3)
-        o_rope(3)
-        o_add(3)
-        o_qn(3, 0, "s")
-        o_qn(3, 1, "s")
-        st_qn(1, 2, 2)
-        st_small(1, 0, 4)
-        q_h(4)
-        s1_half(14, 0, "s")
-        s1_half(14, 1, "v")
-        s1_half(15, 0, "s")
-        s1_half(15, 1, "v")
-        q_ql(14)
-        q_ql(15)
-        o_begin(4)
-        o_kv(4, "s")
-        st_kvn(2, 0, 2)
-        o_qr(4)
-        o_rope(4)
-        o_add(4)
-        o_qn(4, 0, "s")
-        o_qn(4, 1, "s")
-        st_qn(2, 0, 2)
-        o_begin(5)
-        o_kv(5, "s")
-        st_kvn(2, 2, 2)
-        o_qr(5)
-        o_rope(5)
-        o_add(5)
-        o_qn(5, 0, "s")
-        o_qn(5, 1, "s")
-        st_qn(2, 2, 2)
-        st_small(2, 0, 4)
-        tr_h(5, "v", "s")
-        s1_half(16, 0, "s")
-        s1_half(16, 1, "s")
-        s1_half(17, 0, "s")
-        s1_half(17, 1, "v")
-        q_ql(16)
-        q_ql(17)
-        o_begin(6)
-        o_kv(6, "s")
-        st_kvn(3, 0, 2)
-        o_qr(6)
-        o_rope(6)
-        o_add(6)
-        o_qn(6, 0, "s")
-        o_qn(6, 1, "s")
-        st_qn(3, 0, 2)
-        q_h(5)
-        s1_half(18, 0, "s")
-        s1_half(18, 1, "v")
-        s1_half(19, 0, "s")
-        s1_half(19, 1, "v")
-        q_ql(18)
-        q_ql(19)
-        o_begin(7)
-        o_kv(7, "s")
-        st_kvn(3, 2, 2)
-        o_qr(7)
-        o_rope(7)
-        o_add(7)
-        o_qn(7, 0, "s")
-        o_qn(7, 1, "s")
-        st_qn(3, 2, 2)
-        st_small(3, 0, 4)
-        o_begin(8)
-        o_kv(8, "s")
-        st_kvn(4, 0, 2)
-        o_qr(8)
-        o_rope(8)
-        o_add(8)
-        o_qn(8, 0, "s")
-        o_qn(8, 1, "s")
-        st_qn(4, 0, 2)
-        tr_h(6, "v", "s")
-        s1_half(20, 0, "s")
-        s1_half(20, 1, "s")
-        s1_half(21, 0, "s")
-        s1_half(21, 1, "v")
-        q_ql(20)
-        q_ql(21)
-        o_begin(9)
-        o_kv(9, "s")
-        st_kvn(4, 2, 2)
-        o_qr(9)
-        o_rope(9)
-        o_add(9)
-        o_qn(9, 0, "s")
-        o_qn(9, 1, "s")
-        st_qn(4, 2, 2)
-        st_small(4, 0, 4)
-        q_h(6)
-        s1_half(22, 0, "s")
-        s1_half(22, 1, "v")
-        s1_half(23, 0, "s")
-        s1_half(23, 1, "v")
-        q_ql(22)
-        q_ql(23)
-        o_begin(10)
-        o_kv(10, "s")
-        st_kvn(5, 0, 2)
-        o_qr(10)
-        o_rope(10)
-        o_add(10)
-        o_qn(10, 0, "s")
-        o_qn(10, 1, "s")
-        st_qn(5, 0, 2)
-        tr_h(7, "v", "s")
-        s1_half(24, 0, "s")
-        s1_half(24, 1, "s")
-        s1_half(25, 0, "s")
-        s1_half(25, 1, "v")
-        q_ql(24)
-        q_ql(25)
-        o_begin(11)
-        o_kv(11, "s")
-        st_kvn(5, 2, 2)
-        o_qr(11)
-        o_rope(11)
-        o_add(11)
-        o_qn(11, 0, "s")
-        o_qn(11, 1, "s")
-        st_qn(5, 2, 2)
-        st_small(5, 0, 4)
-        q_h(7)
-        s1_half(26, 0, "s")
-        s1_half(26, 1, "v")
-        s1_half(27, 0, "s")
-        s1_half(27, 1, "v")
-        q_ql(26)
-        q_ql(27)
-        o_begin(12)
-        o_kv(12, "s")
-        st_kvn(6, 0, 2)
-        o_qr(12)
-        o_rope(12)
-        o_add(12)
-        o_qn(12, 0, "s")
-        st_qn(6, 0, 1)
-        o_qn(12, 1, "s")
-        st_qn(6, 1, 1)
-        s1_half(28, 0, "s")
-        s1_half(28, 1, "s")
-        s1_half(29, 0, "s")
-        s1_half(29, 1, "v")
-        q_ql(28)
-        q_ql(29)
-        o_begin(13)
-        o_kv(13, "s")
-        st_kvn(6, 2, 2)
-        o_qr(13)
-        o_rope(13)
-        o_add(13)
-        o_qn(13, 0, "s")
-        st_qn(6, 2, 1)
-        o_qn(13, 1, "s")
-        st_qn(6, 3, 1)
-        st_small(6, 0, 4)
-        s1_half(30, 0, "s")
-        s1_half(30, 1, "v")
-        s1_half(31, 0, "s")
-        s1_half(31, 1, "v")
-        q_ql(30)
-        q_ql(31)
-        o_begin(14)
-        o_kv(14, "s")
-        st_kvn(7, 0, 2)
-        o_qr(14)
-        o_rope(14)
-        o_add(14)
-        o_qn(14, 0, "s")
-        st_qn(7, 0, 1)
-        o_qn(14, 1, "s")
-        st_qn(7, 1, 1)
-        st_small(7, 0, 2)
-        o_begin(15)
-        o_kv(15, "s")
-        st_kvn(7, 2, 2)
-        o_qr(15)
-        o_rope(15)
-        o_add(15)
-        st_small(7, 2, 2)
-        o_qn(15, 0, "s")
-        st_qn(7, 2, 1)
-        o_qn(15, 1, "s")
-        st_qn(7, 3, 1)
+        finished = 0
+        for q in range(START_PAIRS, PAIRS + 1):
+            ahead = q // 2 + 1
+            prepare = q % 2 == 0 and ahead < CHUNKS
+            if prepare:
+                transpose_h(ahead, (scalar_copy, scalar_copy))
+            if q < PAIRS:
+                q_lora_pair(q)
+                quantise_q_lora(2 * q)
+                quantise_q_lora(2 * q + 1)
+            upto = min(q, finished + 2)
+            for o in range(finished, upto):
+                output_pair(o)
+            finished = upto
+            if prepare:
+                quantise_h(ahead)

@@ -296,7 +296,7 @@ def tile_absorbqkvo_pa_t_kernel(
                     in1=table[:, 2 * q : 2 * q + 2, :].unsqueeze(2).to_broadcast([P, 2, 3, ROT]),
                 )
             vector_copy(out=v_rope[:, pair, :], in_=small_bank[:, :, 3 * ROT : 4 * ROT])
-            adder = nc.vector if q == PAIRS - 1 else nc.gpsimd
+            adder = nc.vector
             for mine, partner in ((slice(0, 32), slice(32, 64)), (slice(32, 64), slice(0, 32))):
                 adder.tensor_tensor(
                     out=rotated[:, :, pair, mine],

@@ -45,6 +45,7 @@ def tile_absorbqkvo_pa_t_kernel(
         ql_pool = ctx.enter_context(tc.tile_pool(name="ql_pool", bufs=6))
         ql_code_pool = ctx.enter_context(tc.tile_pool(name="ql_code_pool", bufs=2 * START_PAIRS + 4))
         out_pool = ctx.enter_context(tc.tile_pool(name="out_pool", bufs=3))
+        kv_pool = ctx.enter_context(tc.tile_pool(name="kv_pool", bufs=START_PAIRS + 2))
         prod_pool = ctx.enter_context(tc.tile_pool(name="prod_pool", bufs=3))
         psum = ctx.enter_context(tc.psum_pool(name="psum", bufs=8))
 
@@ -237,6 +238,31 @@ def tile_absorbqkvo_pa_t_kernel(
             ql_scales[s] = ql_code_pool.tile([P, 2 * P], U8, name="ql_scales", tag="ql_scales", align_bytes=64)
             quantise(ql_codes[s][:], ql_scales[s][:], ql_grouped[s][:])
 
+        def dram_rows(c):
+            return c // 2, slice(512 * (c % 2), 512 * (c % 2) + 512)
+
+        def kv_pass(out, c, j, cols):
+            tok = slice(P * j, P * (j + 1))
+            nc.tensor.matmul_mx(
+                out=out,
+                lhsT=h_codes[c][:, tok].bitcast(FP8X4), lhsT_scale=h_scales[c][:, tok],
+                rhs=wkv_codes[:, cols].bitcast(FP8X4), rhs_scale=wkv_scales[:, cols],
+                start=True, stop=True,
+            )
+
+        def kv_nope_pair(q):
+            c, second = divmod(q, 2)
+            batch, rows = dram_rows(c)
+            kv_nope = kv_pool.tile([P, 2, NOPE], F32, name="kv_nope", tag="kv_nope")
+            kv_nope_bank = psum.tile([P, 2, NOPE], F32, name="bank", tag="bank")
+            for i in range(2):
+                kv_pass(kv_nope_bank[:, i, :], c, 2 * second + i, KV_NOPE)
+            scalar_copy(out=kv_nope[:], in_=kv_nope_bank[:])
+            nc.sync.dma_start(
+                out=out_4[batch, rows, :].rearrange("(p j) f -> p j f", j=4)[:, 2 * second : 2 * second + 2, :],
+                in_=kv_nope[:],
+            )
+
         chunk_out = {}
 
         def q_passes(out, s, codes, scales, width):
@@ -258,32 +284,19 @@ def tile_absorbqkvo_pa_t_kernel(
             if not second:
                 chunk_out[c] = (
                     out_pool.tile([P, 2, 4, NOPE], F32, name="q_nope", tag="q_nope"),
-                    out_pool.tile([P, 4, NOPE], F32, name="kv_nope", tag="kv_nope"),
                     out_pool.tile([P, 3, 4, ROT], F32, name="rotated", tag="rotated"),
                     out_pool.tile([P, 4, ROT], F32, name="v_rope", tag="v_rope"),
                 )
-            q_nope, kv_nope, rotated, v_rope = chunk_out[c]
-            batch = c // 2
-            rows = slice(512 * (c % 2), 512 * (c % 2) + 512)
+            q_nope, rotated, v_rope = chunk_out[c]
+            batch, rows = dram_rows(c)
             q_nope_dram = out_1[batch, :, rows, :].rearrange("h (p j) f -> p h j f", j=4)
             q_rope_dram = out_0[batch, :, rows, :].rearrange("h (p j) f -> p h j f", j=4)
             k_rope_dram = out_2[batch, rows, :].rearrange("(p j) f -> p j f", j=4)
             v_rope_dram = out_3[batch, rows, :].rearrange("(p j) f -> p j f", j=4)
-            kv_nope_dram = out_4[batch, rows, :].rearrange("(p j) f -> p j f", j=4)
 
             small_bank = psum.tile([P, 2, 4 * ROT], F32, name="bank", tag="bank")
-            kv_nope_bank = psum.tile([P, 2, NOPE], F32, name="bank", tag="bank")
             for i in range(2):
-                tok = slice(P * (j0 + i), P * (j0 + i + 1))
-                for out, cols in ((small_bank[:, i, 2 * ROT : 4 * ROT], KV_ROT), (kv_nope_bank[:, i, :], KV_NOPE)):
-                    nc.tensor.matmul_mx(
-                        out=out,
-                        lhsT=h_codes[c][:, tok].bitcast(FP8X4), lhsT_scale=h_scales[c][:, tok],
-                        rhs=wkv_codes[:, cols].bitcast(FP8X4), rhs_scale=wkv_scales[:, cols],
-                        start=True, stop=True,
-                    )
-            scalar_copy(out=kv_nope[:, pair, :], in_=kv_nope_bank[:])
-            nc.sync.dma_start(out=kv_nope_dram[:, pair, :], in_=kv_nope[:, pair, :])
+                kv_pass(small_bank[:, i, 2 * ROT : 4 * ROT], c, j0 + i, KV_ROT)
             for i in range(2):
                 q_passes(small_bank[:, i, 0 : 2 * ROT], 2 * q + i, rot_codes, rot_scales, 2 * ROT)
 
@@ -296,7 +309,7 @@ def tile_absorbqkvo_pa_t_kernel(
                     in1=table[:, 2 * q : 2 * q + 2, :].unsqueeze(2).to_broadcast([P, 2, 3, ROT]),
                 )
             vector_copy(out=v_rope[:, pair, :], in_=small_bank[:, :, 3 * ROT : 4 * ROT])
-            adder = nc.vector
+            adder = nc.vector if q == PAIRS - 1 else nc.gpsimd
             for mine, partner in ((slice(0, 32), slice(32, 64)), (slice(32, 64), slice(0, 32))):
                 adder.tensor_tensor(
                     out=rotated[:, :, pair, mine],
@@ -347,6 +360,8 @@ def tile_absorbqkvo_pa_t_kernel(
         q_lora_pair(3)
         for s in range(4, 8):
             quantise_q_lora(s)
+        for q in range(START_PAIRS):
+            kv_nope_pair(q)
 
         finished = 0
         for q in range(START_PAIRS, PAIRS + 1):
@@ -358,6 +373,7 @@ def tile_absorbqkvo_pa_t_kernel(
                 q_lora_pair(q)
                 quantise_q_lora(2 * q)
                 quantise_q_lora(2 * q + 1)
+                kv_nope_pair(q)
             upto = min(q, finished + 2)
             for o in range(finished, upto):
                 output_pair(o)

@@ -45,6 +45,7 @@ def tile_absorbqkvo_pa_t_kernel(
         ql_pool = ctx.enter_context(tc.tile_pool(name="ql_pool", bufs=6))
         ql_code_pool = ctx.enter_context(tc.tile_pool(name="ql_code_pool", bufs=2 * START_PAIRS + 4))
         out_pool = ctx.enter_context(tc.tile_pool(name="out_pool", bufs=3))
+        q_nope_pool = ctx.enter_context(tc.tile_pool(name="q_nope_pool", bufs=6))
         kv_pool = ctx.enter_context(tc.tile_pool(name="kv_pool", bufs=START_PAIRS + 2))
         prod_pool = ctx.enter_context(tc.tile_pool(name="prod_pool", bufs=3))
         psum = ctx.enter_context(tc.psum_pool(name="psum", bufs=8))
@@ -64,10 +65,10 @@ def tile_absorbqkvo_pa_t_kernel(
         sin_sb = const.tile([P, TILES, ROT], BF16, name="sin_sb", tag="sin_sb")
         partner_sin = const.tile([P, TILES, ROT], BF16, name="partner_sin", tag="partner_sin")
 
-        def load_h(c):
+        def load_h(c, first=0, count=4):
             nc.sync.dma_start(
-                out=h_sb[c][:],
-                in_=h_rows[512 * c : 512 * (c + 1), :].rearrange("(p j) k -> p (j k)", j=4),
+                out=h_sb[c][:, HID * first : HID * (first + count)].rearrange("p (j k) -> p j k", k=HID),
+                in_=h_rows[512 * c : 512 * (c + 1), :].rearrange("(p j) k -> p j k", j=4)[:, first : first + count, :],
             )
 
         def load_table(table, rows, half):
@@ -79,35 +80,34 @@ def tile_absorbqkvo_pa_t_kernel(
         wqa_rows = w_qa.rearrange("(m r e) k -> r m (e k)", m=4, r=P, e=2)
         wqa_parts = wqa_sb[:].rearrange("p (m x) -> p m x", m=4)
 
-        load_h(0)
+        load_h(0, 0, 2)
         for m in range(4):
             nc.sync.dma_start(out=wqa_parts[:, m, :], in_=wqa_rows[:, m, :])
+        load_h(0, 2, 2)
+        wqb_parts = wqb_sb[:].rearrange("p (a k) -> p a k", a=5)
+        wqb_rows = w_qb.rearrange("(a r) k -> r a k", a=5)
+        for part in (slice(0, 2), slice(2, 5)):
+            nc.sync.dma_start(out=wqb_parts[:, part, :], in_=wqb_rows[:, part, :])
         load_h(1)
         nc.sync.dma_start(
             out=wkv_sb[:].rearrange("p (a k) -> p a k", a=3), in_=w_kv.rearrange("(a r) k -> r a k", a=3)
         )
-        nc.sync.dma_start(
-            out=wqb_sb[:].rearrange("p (a k) -> p a k", a=5), in_=w_qb.rearrange("(a r) k -> r a k", a=5)
-        )
-        load_h(2)
         load_table(sin_sb, sin_rows, 0)
         load_table(cos_sb, cos_rows, 0)
+        load_h(2)
         load_h(3)
         load_table(sin_sb, sin_rows, 1)
         load_table(cos_sb, cos_rows, 1)
         for c in range(4, CHUNKS):
             load_h(c)
 
-        for half in range(2):
+        def prepare_sin(half):
             tiles = slice(16 * half, 16 * (half + 1))
-            nc.gpsimd.tensor_scalar(
-                out=partner_sin[:, tiles, 0:32], in0=sin_sb[:, tiles, 32:64],
-                scalar1=1.0, scalar2=0.0, op0=MULT, op1=ADD,
-            )
-            nc.gpsimd.tensor_scalar(
-                out=partner_sin[:, tiles, 32:64], in0=sin_sb[:, tiles, 0:32],
-                scalar1=-1.0, scalar2=0.0, op0=MULT, op1=ADD,
-            )
+            for out, src, sign in ((slice(0, 32), slice(32, 64), 1.0), (slice(32, 64), slice(0, 32), -1.0)):
+                nc.vector.tensor_scalar(
+                    out=partner_sin[:, tiles, out], in0=sin_sb[:, tiles, src],
+                    scalar1=sign, scalar2=0.0, op0=MULT, op1=ADD,
+                )
 
         def transposed(words, starts):
             bank = new_bank()
@@ -131,16 +131,21 @@ def tile_absorbqkvo_pa_t_kernel(
         h_codes = {}
         h_scales = {}
 
-        def transpose_h(c, copies):
-            h_grouped[c] = grouped_pool.tile([P, 4 * BANK], BF16, name="h_grouped", tag="h_grouped", align_bytes=64)
-            dst = word_view(h_grouped[c], 4)
-            for b in range(2):
-                bank = transposed(h_sb[c][:].bitcast(F32), row_blocks(2 * b, 2, HID // 2))
-                regroup(copies[b], dst[:, 2 * b : 2 * b + 2], bank, 2)
+        def transpose_h(q, copy):
+            c, b = divmod(q, 2)
+            if b == 0:
+                h_grouped[c] = grouped_pool.tile([P, 4 * BANK], BF16, name="h_grouped", tag="h_grouped", align_bytes=64)
+                h_codes[c] = h_code_pool.tile([P, BANK], U32, name="h_codes", tag="h_codes", align_bytes=64)
+                h_scales[c] = h_code_pool.tile([P, BANK], U8, name="h_scales", tag="h_scales", align_bytes=64)
+            bank = transposed(h_sb[c][:].bitcast(F32), row_blocks(2 * b, 2, HID // 2))
+            regroup(copy, word_view(h_grouped[c], 4)[:, 2 * b : 2 * b + 2], bank, 2)
 
-        def quantise_h(c):
-            h_codes[c] = h_code_pool.tile([P, BANK], U32, name="h_codes", tag="h_codes", align_bytes=64)
-            h_scales[c] = h_code_pool.tile([P, BANK], U8, name="h_scales", tag="h_scales", align_bytes=64)
+        def quantise_h(q):
+            c, b = divmod(q, 2)
+            cols = slice(2 * P * b, 2 * P * (b + 1))
+            quantise(h_codes[c][:, cols], h_scales[c][:, cols], h_grouped[c][:, 2 * BANK * b : 2 * BANK * (b + 1)])
+
+        def quantise_h_chunk(c):
             quantise(h_codes[c][:], h_scales[c][:], h_grouped[c][:])
 
         wqa_grouped = const.tile([P, 8 * BANK], BF16, name="wqa_grouped", tag="wqa_grouped", align_bytes=64)
@@ -178,14 +183,13 @@ def tile_absorbqkvo_pa_t_kernel(
         rot_codes = const.tile([P, 2 * P], U32, name="rot_codes", tag="rot_codes", align_bytes=64)
         rot_scales = const.tile([P, 2 * P], U8, name="rot_scales", tag="rot_scales", align_bytes=64)
 
-        def transpose_wqb():
+        def transpose_wqb(first, copies):
             nope_dst = nope_grouped[:].bitcast(F32).rearrange("p (g n u) -> p g n u", g=2, u=2)
             rot_dst = rot_grouped[:].bitcast(F32).rearrange("p (g n u) -> p g n u", g=2, u=2)
             words = wqb_sb[:].bitcast(F32)
-            for a in range(5):
+            for a, copy in enumerate(copies, first):
                 bank = transposed(words, [QLR // 2 * a + 2 * P * g + P * u for g in range(2) for u in range(2)])
                 src = bank[:].rearrange("p (g u r) -> p g r u", g=2, u=2)
-                copy = vector_copy if a % 2 else scalar_copy
                 for head in range(2):
                     for first, count, dst, col in (
                         (HEAD * head, ROT, rot_dst, ROT * head),
@@ -199,11 +203,12 @@ def tile_absorbqkvo_pa_t_kernel(
                                 in_=src[:, :, lo - P * a : hi - P * a, :],
                             )
 
-        def quantise_wqb():
+        def quantise_nope(g):
+            cols = slice(BANK * g, BANK * (g + 1))
+            quantise(nope_codes[:, cols], nope_scales[:, cols], nope_grouped[:, 4 * BANK * g : 4 * BANK * (g + 1)])
+
+        def quantise_rot():
             quantise(rot_codes[:], rot_scales[:], rot_grouped[:])
-            for g in range(2):
-                cols = slice(BANK * g, BANK * (g + 1))
-                quantise(nope_codes[:, cols], nope_scales[:, cols], nope_grouped[:, 4 * BANK * g : 4 * BANK * (g + 1)])
 
         ql_grouped = {}
         ql_codes = {}
@@ -228,10 +233,13 @@ def tile_absorbqkvo_pa_t_kernel(
                 in_=bank[:].rearrange("p (t r) -> p r t", t=4),
             )
 
-        def q_lora_pair(q):
-            for s in (2 * q, 2 * q + 1):
-                q_lora_bank(s, 0, scalar_copy)
-                q_lora_bank(s, 1, vector_copy)
+        def q_lora_pair(q, copies=(scalar_copy, vector_copy, scalar_copy, vector_copy)):
+            for i, copy in enumerate(copies):
+                q_lora_bank(2 * q + i // 2, i % 2, copy)
+
+        def q_lora_g(q, g, copies):
+            for i, copy in enumerate(copies):
+                q_lora_bank(2 * q + i, g, copy)
 
         def quantise_q_lora(s):
             ql_codes[s] = ql_code_pool.tile([P, 2 * P], U32, name="ql_codes", tag="ql_codes", align_bytes=64)
@@ -276,107 +284,137 @@ def tile_absorbqkvo_pa_t_kernel(
                     start=(g == 0), stop=(g == 1),
                 )
 
-        def output_pair(q):
-            c, second = divmod(q, 2)
-            j0 = 2 * second
-            pair = slice(j0, j0 + 2)
-            last_chunk = c == CHUNKS - 1
-            if not second:
-                chunk_out[c] = (
-                    out_pool.tile([P, 2, 4, NOPE], F32, name="q_nope", tag="q_nope"),
-                    out_pool.tile([P, 3, 4, ROT], F32, name="rotated", tag="rotated"),
-                    out_pool.tile([P, 4, ROT], F32, name="v_rope", tag="v_rope"),
-                )
-            q_nope, rotated, v_rope = chunk_out[c]
-            batch, rows = dram_rows(c)
-            q_nope_dram = out_1[batch, :, rows, :].rearrange("h (p j) f -> p h j f", j=4)
-            q_rope_dram = out_0[batch, :, rows, :].rearrange("h (p j) f -> p h j f", j=4)
-            k_rope_dram = out_2[batch, rows, :].rearrange("(p j) f -> p j f", j=4)
-            v_rope_dram = out_3[batch, rows, :].rearrange("(p j) f -> p j f", j=4)
-
-            small_bank = psum.tile([P, 2, 4 * ROT], F32, name="bank", tag="bank")
-            for i in range(2):
-                kv_pass(small_bank[:, i, 2 * ROT : 4 * ROT], c, j0 + i, KV_ROT)
-            for i in range(2):
-                q_passes(small_bank[:, i, 0 : 2 * ROT], 2 * q + i, rot_codes, rot_scales, 2 * ROT)
-
-            x = small_bank[:, :, 0 : 3 * ROT].rearrange("p j (n f) -> p j n f", n=3)
-            by_cos = prod_pool.tile([P, 2, 3, ROT], F32, name="by_cos", tag="by_cos")
-            by_sin = prod_pool.tile([P, 2, 3, ROT], F32, name="by_sin", tag="by_sin")
+        def rotate(out, x, tiles, heads, adder):
+            count = tiles.stop - tiles.start
+            by_cos = prod_pool.tile([P, count, heads, ROT], F32, name="by_cos", tag="by_cos%d" % heads)
+            by_sin = prod_pool.tile([P, count, heads, ROT], F32, name="by_sin", tag="by_sin%d" % heads)
             for prod, table in ((by_cos, cos_sb), (by_sin, partner_sin)):
                 nc.vector.tensor_tensor(
                     out=prod[:], in0=x, op=MULT,
-                    in1=table[:, 2 * q : 2 * q + 2, :].unsqueeze(2).to_broadcast([P, 2, 3, ROT]),
+                    in1=table[:, tiles, :].unsqueeze(2).to_broadcast([P, count, heads, ROT]),
                 )
-            vector_copy(out=v_rope[:, pair, :], in_=small_bank[:, :, 3 * ROT : 4 * ROT])
-            adder = nc.vector if q == PAIRS - 1 else nc.gpsimd
             for mine, partner in ((slice(0, 32), slice(32, 64)), (slice(32, 64), slice(0, 32))):
                 adder.tensor_tensor(
-                    out=rotated[:, :, pair, mine],
+                    out=out[:, :, :, mine],
                     in0=by_cos[:, :, :, mine].rearrange("p j n f -> p n j f"),
                     in1=by_sin[:, :, :, partner].rearrange("p j n f -> p n j f"),
                     op=ADD,
                 )
 
+        def kv_rot_chunk(c):
+            batch, rows = dram_rows(c)
+            bank = psum.tile([P, 4, 2 * ROT], F32, name="bank", tag="bank")
+            for j in range(4):
+                kv_pass(bank[:, j, :], c, j, KV_ROT)
+            k_rope = out_pool.tile([P, 1, 4, ROT], F32, name="k_rope", tag="k_rope")
+            v_rope = out_pool.tile([P, 4, ROT], F32, name="v_rope", tag="v_rope")
+            rotate(k_rope, bank[:, :, 0:ROT].unsqueeze(2), slice(4 * c, 4 * c + 4), 1, nc.gpsimd)
+            vector_copy(out=v_rope[:], in_=bank[:, :, ROT : 2 * ROT])
+            nc.sync.dma_start(out=out_3[batch, rows, :].rearrange("(p j) f -> p j f", j=4), in_=v_rope[:])
+            nc.sync.dma_start(out=out_2[batch, rows, :].rearrange("(p j) f -> p j f", j=4), in_=k_rope[:, 0, :, :])
+
+        def rope_pair(q):
+            c, second = divmod(q, 2)
+            if not second:
+                chunk_out[c] = out_pool.tile([P, 2, 4, ROT], F32, name="q_rope", tag="q_rope")
+            bank = psum.tile([P, 2, 2, ROT], F32, name="bank", tag="bank")
             for i in range(2):
-                j = j0 + i
+                q_passes(bank[:, i, :, :].rearrange("p n f -> p (n f)"), 2 * q + i, rot_codes, rot_scales, 2 * ROT)
+            rotate(chunk_out[c][:, :, 2 * second : 2 * second + 2, :], bank[:], slice(2 * q, 2 * q + 2), 2, nc.vector if q == PAIRS - 1 else nc.gpsimd)
+
+        def store_rope(q):
+            c, second = divmod(q, 2)
+            batch, rows = dram_rows(c)
+            last_chunk = c == CHUNKS - 1
+            if last_chunk or second:
+                done = slice(2 * second, 2 * second + 2) if last_chunk else slice(0, 4)
+                q_rope_dram = out_0[batch, :, rows, :].rearrange("h (p j) f -> p h j f", j=4)
+                nc.sync.dma_start(out=q_rope_dram[:, :, done, :], in_=chunk_out[c][:, :, done, :])
+
+        def nope_pair(q):
+            c, second = divmod(q, 2)
+            j0 = 2 * second
+            pair = slice(j0, j0 + 2)
+            last_pair = q == PAIRS - 1
+            batch, rows = dram_rows(c)
+            q_nope = q_nope_pool.tile([P, 2, 2, NOPE], F32, name="q_nope", tag="q_nope")
+            q_nope_dram = out_1[batch, :, rows, :].rearrange("h (p j) f -> p h j f", j=4)
+            for i in range(2):
                 nope_bank = new_bank()
                 q_passes(nope_bank[:], 2 * q + i, nope_codes, nope_scales, BANK)
-                scalar_copy(out=q_nope[:, :, j, :], in_=nope_bank[:].rearrange("p (h f) -> p h f", h=2))
-                if last_chunk:
-                    nc.sync.dma_start(out=q_nope_dram[:, :, j : j + 1, :], in_=q_nope[:, :, j : j + 1, :])
-            if not last_chunk:
-                nc.sync.dma_start(out=q_nope_dram[:, :, pair, :], in_=q_nope[:, :, pair, :])
-            if last_chunk or second:
-                done = pair if last_chunk else slice(0, 4)
-                nc.sync.dma_start(out=v_rope_dram[:, done, :], in_=v_rope[:, done, :])
-                nc.sync.dma_start(out=q_rope_dram[:, :, done, :], in_=rotated[:, 0:2, done, :])
-                nc.sync.dma_start(out=k_rope_dram[:, done, :], in_=rotated[:, 2, done, :])
+                scalar_copy(out=q_nope[:, :, i, :], in_=nope_bank[:].rearrange("p (h f) -> p h f", h=2))
+                if last_pair:
+                    nc.sync.dma_start(out=q_nope_dram[:, :, j0 + i : j0 + i + 1, :], in_=q_nope[:, :, i : i + 1, :])
+            if not last_pair:
+                nc.sync.dma_start(out=q_nope_dram[:, :, pair, :], in_=q_nope[:])
 
-        transpose_h(0, (vector_copy, scalar_copy))
-        transpose_wqa(0, scalar_copy)
+
+        V = vector_copy
+        A = scalar_copy
+        transpose_h(0, V)
+        transpose_wqa(0, A)
         quantise_h(0)
-        for m in range(1, 4):
-            transpose_wqa(m, vector_copy if m % 2 else scalar_copy)
-            quantise_wqa(m - 1)
+        transpose_wqa(1, V)
+        quantise_wqa(0)
+        transpose_wqa(2, A)
+        quantise_wqa(1)
+        transpose_wqa(3, A)
+        quantise_wqa(2)
         quantise_wqa(3)
-        for j in range(4):
-            q_lora_bank(j, 0, vector_copy if j % 2 else scalar_copy)
-        transpose_h(1, (vector_copy, scalar_copy))
+        q_lora_g(0, 0, (A, V))
+        q_lora_g(0, 1, (A, V))
+        transpose_h(1, A)
+        quantise_h(1)
+        transpose_wqb(0, (A, V))
+        quantise_q_lora(0)
+        quantise_q_lora(1)
+        transpose_wqb(2, (A, A, V))
+        q_lora_g(1, 0, (A, A))
+        quantise_nope(0)
+        quantise_nope(1)
+        q_lora_g(1, 1, (A, V))
+        transpose_h(2, A)
+        transpose_h(3, V)
         transpose_wkv()
-        for j in range(4):
-            q_lora_bank(j, 1, scalar_copy if j % 2 else vector_copy)
-            if j == 0:
-                quantise_h(1)
-            else:
-                quantise_q_lora(j - 1)
+        quantise_q_lora(2)
         quantise_q_lora(3)
-        q_lora_pair(2)
-        transpose_wqb()
-        transpose_h(2, (vector_copy, scalar_copy))
-        quantise_h(2)
+        quantise_h_chunk(1)
+        nope_pair(0)
+        nope_pair(1)
         quantise_wkv()
-        quantise_wqb()
-        q_lora_pair(3)
-        for s in range(4, 8):
-            quantise_q_lora(s)
-        for q in range(START_PAIRS):
-            kv_nope_pair(q)
+        quantise_rot()
+        q_lora_pair(2)
+        prepare_sin(0)
+        kv_nope_pair(0)
+        rope_pair(0)
+        kv_rot_chunk(0)
+        quantise_q_lora(4)
+        quantise_q_lora(5)
+        transpose_h(4,A)
+        transpose_h(5,A)
+        rope_pair(1)
+        store_rope(1)
+        kv_nope_pair(1)
+        kv_nope_pair(2)
+        quantise_h_chunk(2)
 
-        finished = 0
-        for q in range(START_PAIRS, PAIRS + 1):
+        for q in range(3, PAIRS + 1):
             ahead = q // 2 + 1
-            prepare = q % 2 == 0 and ahead < CHUNKS
+            prepare = q % 2 == 0 and 3 <= ahead < CHUNKS
             if prepare:
-                transpose_h(ahead, (scalar_copy, scalar_copy))
+                transpose_h(2 * ahead, A)
+                transpose_h(2 * ahead + 1, A)
             if q < PAIRS:
                 q_lora_pair(q)
                 quantise_q_lora(2 * q)
                 quantise_q_lora(2 * q + 1)
                 kv_nope_pair(q)
-            upto = min(q, finished + 2)
-            for o in range(finished, upto):
-                output_pair(o)
-            finished = upto
+            rope_pair(q - 1)
+            nope_pair(q - 1)
+            store_rope(q - 1)
+            if q % 2 and q < PAIRS:
+                kv_rot_chunk(q // 2)
             if prepare:
-                quantise_h(ahead)
+                quantise_h_chunk(ahead)
+                if ahead == 4:
+                    prepare_sin(1)

@@ -41,12 +41,12 @@ def tile_absorbqkvo_pa_t_kernel(
         const = ctx.enter_context(tc.tile_pool(name="const", bufs=1))
         h_pool = ctx.enter_context(tc.tile_pool(name="h_pool", bufs=CHUNKS))
         grouped_pool = ctx.enter_context(tc.tile_pool(name="grouped_pool", bufs=2))
-        h_code_pool = ctx.enter_context(tc.tile_pool(name="h_code_pool", bufs=4))
+        h_code_pool = ctx.enter_context(tc.tile_pool(name="h_code_pool", bufs=7))
         ql_pool = ctx.enter_context(tc.tile_pool(name="ql_pool", bufs=6))
         ql_code_pool = ctx.enter_context(tc.tile_pool(name="ql_code_pool", bufs=2 * START_PAIRS + 4))
         out_pool = ctx.enter_context(tc.tile_pool(name="out_pool", bufs=3))
-        q_nope_pool = ctx.enter_context(tc.tile_pool(name="q_nope_pool", bufs=6))
-        kv_pool = ctx.enter_context(tc.tile_pool(name="kv_pool", bufs=START_PAIRS + 2))
+        q_nope_pool = ctx.enter_context(tc.tile_pool(name="q_nope_pool", bufs=4))
+        kv_pool = ctx.enter_context(tc.tile_pool(name="kv_pool", bufs=3))
         prod_pool = ctx.enter_context(tc.tile_pool(name="prod_pool", bufs=3))
         psum = ctx.enter_context(tc.psum_pool(name="psum", bufs=8))
 
@@ -258,20 +258,28 @@ def tile_absorbqkvo_pa_t_kernel(
                 start=True, stop=True,
             )
 
+        chunk_kv = {}
+
         def kv_nope_pair(q):
             c, second = divmod(q, 2)
             batch, rows = dram_rows(c)
-            kv_nope = kv_pool.tile([P, 2, NOPE], F32, name="kv_nope", tag="kv_nope")
+            if not second:
+                chunk_kv[c] = kv_pool.tile([P, 4, NOPE], F32, name="kv_nope", tag="kv_nope")
+            kv_nope = chunk_kv[c]
             kv_nope_bank = psum.tile([P, 2, NOPE], F32, name="bank", tag="bank")
             for i in range(2):
                 kv_pass(kv_nope_bank[:, i, :], c, 2 * second + i, KV_NOPE)
-            scalar_copy(out=kv_nope[:], in_=kv_nope_bank[:])
-            nc.sync.dma_start(
-                out=out_4[batch, rows, :].rearrange("(p j) f -> p j f", j=4)[:, 2 * second : 2 * second + 2, :],
-                in_=kv_nope[:],
-            )
+            scalar_copy(out=kv_nope[:, 2 * second : 2 * second + 2, :], in_=kv_nope_bank[:])
+            kv_dram = out_4[batch, rows, :].rearrange("(p j) f -> p j f", j=4)
+            if c < 5:
+                if second:
+                    nc.sync.dma_start(out=kv_dram, in_=kv_nope[:])
+            else:
+                pair = slice(2 * second, 2 * second + 2)
+                nc.sync.dma_start(out=kv_dram[:, pair, :], in_=kv_nope[:, pair, :])
 
         chunk_out = {}
+        chunk_nope = {}
 
         def q_passes(out, s, codes, scales, width):
             for g in range(2):
@@ -326,8 +334,8 @@ def tile_absorbqkvo_pa_t_kernel(
             c, second = divmod(q, 2)
             batch, rows = dram_rows(c)
             last_chunk = c == CHUNKS - 1
-            if last_chunk or second:
-                done = slice(2 * second, 2 * second + 2) if last_chunk else slice(0, 4)
+            if second:
+                done = slice(0, 4)
                 q_rope_dram = out_0[batch, :, rows, :].rearrange("h (p j) f -> p h j f", j=4)
                 nc.sync.dma_start(out=q_rope_dram[:, :, done, :], in_=chunk_out[c][:, :, done, :])
 
@@ -335,19 +343,20 @@ def tile_absorbqkvo_pa_t_kernel(
             c, second = divmod(q, 2)
             j0 = 2 * second
             pair = slice(j0, j0 + 2)
-            last_pair = q == PAIRS - 1
             batch, rows = dram_rows(c)
-            q_nope = q_nope_pool.tile([P, 2, 2, NOPE], F32, name="q_nope", tag="q_nope")
+            if not second:
+                chunk_nope[c] = q_nope_pool.tile([P, 2, 4, NOPE], F32, name="q_nope", tag="q_nope")
+            q_nope = chunk_nope[c]
             q_nope_dram = out_1[batch, :, rows, :].rearrange("h (p j) f -> p h j f", j=4)
             for i in range(2):
                 nope_bank = new_bank()
                 q_passes(nope_bank[:], 2 * q + i, nope_codes, nope_scales, BANK)
-                scalar_copy(out=q_nope[:, :, i, :], in_=nope_bank[:].rearrange("p (h f) -> p h f", h=2))
-                if last_pair:
-                    nc.sync.dma_start(out=q_nope_dram[:, :, j0 + i : j0 + i + 1, :], in_=q_nope[:, :, i : i + 1, :])
-            if not last_pair:
-                nc.sync.dma_start(out=q_nope_dram[:, :, pair, :], in_=q_nope[:])
-
+                scalar_copy(out=q_nope[:, :, j0 + i, :], in_=nope_bank[:].rearrange("p (h f) -> p h f", h=2))
+            if c < 5:
+                if second:
+                    nc.sync.dma_start(out=q_nope_dram, in_=q_nope[:])
+            else:
+                nc.sync.dma_start(out=q_nope_dram[:, :, pair, :], in_=q_nope[:, :, pair, :])
 
         V = vector_copy
         A = scalar_copy
@@ -398,23 +407,32 @@ def tile_absorbqkvo_pa_t_kernel(
         kv_nope_pair(2)
         quantise_h_chunk(2)
 
+        prepared = 2
+        kv_done = 3
+        kv_target = [min(PAIRS, q + 1 + (q - 3) // 2) for q in range(PAIRS + 3)]
+        fresh = []
         for q in range(3, PAIRS + 1):
-            ahead = q // 2 + 1
-            prepare = q % 2 == 0 and 3 <= ahead < CHUNKS
-            if prepare:
-                transpose_h(2 * ahead, A)
-                transpose_h(2 * ahead + 1, A)
+            new = range(prepared + 1, (kv_target[q + 2] - 1) // 2 + 1)
+            for c in new:
+                transpose_h(2 * c, A)
+                transpose_h(2 * c + 1, A)
             if q < PAIRS:
                 q_lora_pair(q)
                 quantise_q_lora(2 * q)
                 quantise_q_lora(2 * q + 1)
-                kv_nope_pair(q)
+            for c in fresh:
+                quantise_h_chunk(c)
+            fresh = new
+            for p in range(kv_done, kv_target[q]):
+                kv_nope_pair(p)
             rope_pair(q - 1)
             nope_pair(q - 1)
             store_rope(q - 1)
-            if q % 2 and q < PAIRS:
-                kv_rot_chunk(q // 2)
-            if prepare:
-                quantise_h_chunk(ahead)
-                if ahead == 4:
+            for p in range(kv_done, kv_target[q]):
+                if p % 2:
+                    kv_rot_chunk(p // 2)
+            kv_done = kv_target[q]
+            for c in new:
+                prepared = c
+                if c == 4:
                     prepare_sin(1)

from contextlib import ExitStack

import concourse.mybir as mybir
from concourse.masks import make_identity

F32 = mybir.dt.float32
BF16 = mybir.dt.bfloat16
U32 = mybir.dt.uint32
U8 = mybir.dt.uint8
FP8X4 = mybir.dt.float8_e4m3fn_x4
MULT = mybir.AluOpType.mult
ADD = mybir.AluOpType.add

P = 128
BANK = 512
TOKENS = 4096
HID = 512
QLR = 1024
ROT = 64
NOPE = 256
HEAD = ROT + NOPE
CHUNKS = TOKENS // 512
PAIRS = 2 * CHUNKS
TILES = 4 * CHUNKS
START_PAIRS = 4
FLOPS = 2 * TOKENS * (HID * QLR + QLR * 2 * HEAD + HID * (2 * ROT + NOPE))


def tile_absorbqkvo_pa_t_kernel(
    tc, hidden_states, cos, sin, w_qa, w_qb, w_kv, out_0, out_1, out_2, out_3, out_4
):
    nc = tc.nc
    h_rows = hidden_states.flatten_outer_dims()
    cos_rows = cos.flatten_outer_dims()
    sin_rows = sin.flatten_outer_dims()
    scalar_copy = nc.scalar.copy
    vector_copy = nc.vector.tensor_copy

    with ExitStack() as ctx:
        ctx.enter_context(tc.manual_schedule())
        const = ctx.enter_context(tc.tile_pool(name="const", bufs=1))
        h_pool = ctx.enter_context(tc.tile_pool(name="h_pool", bufs=CHUNKS))
        grouped_pool = ctx.enter_context(tc.tile_pool(name="grouped_pool", bufs=2))
        h_code_pool = ctx.enter_context(tc.tile_pool(name="h_code_pool", bufs=7))
        ql_pool = ctx.enter_context(tc.tile_pool(name="ql_pool", bufs=6))
        ql_code_pool = ctx.enter_context(tc.tile_pool(name="ql_code_pool", bufs=2 * START_PAIRS + 4))
        out_pool = ctx.enter_context(tc.tile_pool(name="out_pool", bufs=3))
        q_nope_pool = ctx.enter_context(tc.tile_pool(name="q_nope_pool", bufs=4))
        kv_pool = ctx.enter_context(tc.tile_pool(name="kv_pool", bufs=3))
        prod_pool = ctx.enter_context(tc.tile_pool(name="prod_pool", bufs=3))
        psum = ctx.enter_context(tc.psum_pool(name="psum", bufs=8))

        def new_bank():
            bank = psum.tile([P, BANK], F32, name="bank", tag="bank")
            return bank

        identity = const.tile([P, P], F32, name="identity", tag="identity")
        make_identity(nc, identity[:])

        h_sb = [h_pool.tile([P, 4 * HID], BF16, name="h_sb", tag="h_sb") for c in range(CHUNKS)]
        wqa_sb = const.tile([P, 8 * HID], BF16, name="wqa_sb", tag="wqa_sb")
        wkv_sb = const.tile([P, 3 * HID], BF16, name="wkv_sb", tag="wkv_sb")
        wqb_sb = const.tile([P, 5 * QLR], BF16, name="wqb_sb", tag="wqb_sb")
        cos_sb = const.tile([P, TILES, ROT], BF16, name="cos_sb", tag="cos_sb")
        sin_sb = const.tile([P, TILES, ROT], BF16, name="sin_sb", tag="sin_sb")
        partner_sin = const.tile([P, TILES, ROT], BF16, name="partner_sin", tag="partner_sin")

        def load_h(c, first=0, count=4):
            nc.sync.dma_start(
                out=h_sb[c][:, HID * first : HID * (first + count)].rearrange("p (j k) -> p j k", k=HID),
                in_=h_rows[512 * c : 512 * (c + 1), :].rearrange("(p j) k -> p j k", j=4)[:, first : first + count, :],
            )

        def load_table(table, rows, half):
            nc.sync.dma_start(
                out=table[:, 16 * half : 16 * (half + 1), :].rearrange("p (c j) f -> p c (j f)", j=4),
                in_=rows[2048 * half : 2048 * (half + 1), :].rearrange("(c p j) f -> p c (j f)", c=4, p=P, j=4),
            )

        wqa_rows = w_qa.rearrange("(m r e) k -> r m (e k)", m=4, r=P, e=2)
        wqa_parts = wqa_sb[:].rearrange("p (m x) -> p m x", m=4)

        load_h(0, 0, 2)
        for m in range(4):
            nc.sync.dma_start(out=wqa_parts[:, m, :], in_=wqa_rows[:, m, :])
        load_h(0, 2, 2)
        wqb_parts = wqb_sb[:].rearrange("p (a k) -> p a k", a=5)
        wqb_rows = w_qb.rearrange("(a r) k -> r a k", a=5)
        for part in (slice(0, 2), slice(2, 5)):
            nc.sync.dma_start(out=wqb_parts[:, part, :], in_=wqb_rows[:, part, :])
        load_h(1)
        nc.sync.dma_start(
            out=wkv_sb[:].rearrange("p (a k) -> p a k", a=3), in_=w_kv.rearrange("(a r) k -> r a k", a=3)
        )
        load_table(sin_sb, sin_rows, 0)
        load_table(cos_sb, cos_rows, 0)
        load_h(2)
        load_h(3)
        load_table(sin_sb, sin_rows, 1)
        load_table(cos_sb, cos_rows, 1)
        for c in range(4, CHUNKS):
            load_h(c)

        def prepare_sin(half):
            tiles = slice(16 * half, 16 * (half + 1))
            for out, src, sign in ((slice(0, 32), slice(32, 64), 1.0), (slice(32, 64), slice(0, 32), -1.0)):
                nc.vector.tensor_scalar(
                    out=partner_sin[:, tiles, out], in0=sin_sb[:, tiles, src],
                    scalar1=sign, scalar2=0.0, op0=MULT, op1=ADD,
                )

        def transposed(words, starts):
            bank = new_bank()
            for i, start in enumerate(starts):
                nc.tensor.transpose(bank[:, i * P : (i + 1) * P], words[:, start : start + P], identity[:])
            return bank

        def row_blocks(first, count, words_per_row):
            return [words_per_row * (first + a) + P * u for a in range(count) for u in range(2)]

        def word_view(grouped, blocks):
            return grouped[:].bitcast(F32).rearrange("p (a r u) -> p a r u", a=blocks, u=2)

        def regroup(copy, dst, bank, blocks):
            copy(out=dst, in_=bank[:, 0 : 2 * P * blocks].rearrange("p (a u r) -> p a r u", a=blocks, u=2))

        def quantise(codes, scales, grouped):
            nc.vector.quantize_mx(out=codes.bitcast(FP8X4), scales=scales, in_=grouped)

        h_grouped = {}
        h_codes = {}
        h_scales = {}

        def transpose_h(q, copy):
            c, b = divmod(q, 2)
            if b == 0:
                h_grouped[c] = grouped_pool.tile([P, 4 * BANK], BF16, name="h_grouped", tag="h_grouped", align_bytes=64)
                h_codes[c] = h_code_pool.tile([P, BANK], U32, name="h_codes", tag="h_codes", align_bytes=64)
                h_scales[c] = h_code_pool.tile([P, BANK], U8, name="h_scales", tag="h_scales", align_bytes=64)
            bank = transposed(h_sb[c][:].bitcast(F32), row_blocks(2 * b, 2, HID // 2))
            regroup(copy, word_view(h_grouped[c], 4)[:, 2 * b : 2 * b + 2], bank, 2)

        def quantise_h(q):
            c, b = divmod(q, 2)
            cols = slice(2 * P * b, 2 * P * (b + 1))
            quantise(h_codes[c][:, cols], h_scales[c][:, cols], h_grouped[c][:, 2 * BANK * b : 2 * BANK * (b + 1)])

        def quantise_h_chunk(c):
            quantise(h_codes[c][:], h_scales[c][:], h_grouped[c][:])

        wqa_grouped = const.tile([P, 8 * BANK], BF16, name="wqa_grouped", tag="wqa_grouped", align_bytes=64)
        wqa_codes = const.tile([P, 8 * P], U32, name="wqa_codes", tag="wqa_codes", align_bytes=64)
        wqa_scales = const.tile([P, 8 * P], U8, name="wqa_scales", tag="wqa_scales", align_bytes=64)

        def transpose_wqa(m, copy):
            bank = transposed(wqa_sb[:].bitcast(F32), row_blocks(2 * m, 2, HID // 2))
            regroup(copy, word_view(wqa_grouped, 8)[:, 2 * m : 2 * m + 2], bank, 2)

        def quantise_wqa(m):
            cols = slice(2 * P * m, 2 * P * (m + 1))
            quantise(wqa_codes[:, cols], wqa_scales[:, cols], wqa_grouped[:, 2 * BANK * m : 2 * BANK * (m + 1)])

        wkv_grouped = const.tile([P, 3 * BANK], BF16, name="wkv_grouped", tag="wkv_grouped", align_bytes=64)
        wkv_codes = const.tile([P, 3 * P], U32, name="wkv_codes", tag="wkv_codes", align_bytes=64)
        wkv_scales = const.tile([P, 3 * P], U8, name="wkv_scales", tag="wkv_scales", align_bytes=64)
        KV_ROT = slice(0, 2 * ROT)
        KV_NOPE = slice(2 * ROT, 2 * ROT + NOPE)

        def transpose_wkv():
            dst = word_view(wkv_grouped, 3)
            words = wkv_sb[:].bitcast(F32)
            regroup(scalar_copy, dst[:, 0:2], transposed(words, row_blocks(0, 2, HID // 2)), 2)
            regroup(scalar_copy, dst[:, 2:3], transposed(words, row_blocks(2, 1, HID // 2)), 1)

        def quantise_wkv():
            quantise(wkv_codes[:, KV_ROT], wkv_scales[:, KV_ROT], wkv_grouped[:, 0:BANK])
            quantise(wkv_codes[:, KV_NOPE], wkv_scales[:, KV_NOPE], wkv_grouped[:, BANK : 3 * BANK])

        nope_grouped = const.tile([P, 8 * BANK], BF16, name="nope_grouped", tag="nope_grouped", align_bytes=64)
        nope_codes = const.tile([P, 2 * BANK], U32, name="nope_codes", tag="nope_codes", align_bytes=64)
        nope_scales = const.tile([P, 2 * BANK], U8, name="nope_scales", tag="nope_scales", align_bytes=64)
        rot_grouped = const.tile([P, 2 * BANK], BF16, name="rot_grouped", tag="rot_grouped", align_bytes=64)
        rot_codes = const.tile([P, 2 * P], U32, name="rot_codes", tag="rot_codes", align_bytes=64)
        rot_scales = const.tile([P, 2 * P], U8, name="rot_scales", tag="rot_scales", align_bytes=64)

        def transpose_wqb(first, copies):
            nope_dst = nope_grouped[:].bitcast(F32).rearrange("p (g n u) -> p g n u", g=2, u=2)
            rot_dst = rot_grouped[:].bitcast(F32).rearrange("p (g n u) -> p g n u", g=2, u=2)
            words = wqb_sb[:].bitcast(F32)
            for a, copy in enumerate(copies, first):
                bank = transposed(words, [QLR // 2 * a + 2 * P * g + P * u for g in range(2) for u in range(2)])
                src = bank[:].rearrange("p (g u r) -> p g r u", g=2, u=2)
                for head in range(2):
                    for first, count, dst, col in (
                        (HEAD * head, ROT, rot_dst, ROT * head),
                        (HEAD * head + ROT, NOPE, nope_dst, NOPE * head),
                    ):
                        lo = max(first, P * a)
                        hi = min(first + count, P * (a + 1))
                        if lo < hi:
                            copy(
                                out=dst[:, :, col + lo - first : col + hi - first, :],
                                in_=src[:, :, lo - P * a : hi - P * a, :],
                            )

        def quantise_nope(g):
            cols = slice(BANK * g, BANK * (g + 1))
            quantise(nope_codes[:, cols], nope_scales[:, cols], nope_grouped[:, 4 * BANK * g : 4 * BANK * (g + 1)])

        def quantise_rot():
            quantise(rot_codes[:], rot_scales[:], rot_grouped[:])

        ql_grouped = {}
        ql_codes = {}
        ql_scales = {}

        def q_lora_bank(s, g, copy):
            c, j = divmod(s, 4)
            if g == 0:
                ql_grouped[s] = ql_pool.tile([P, 2 * BANK], BF16, name="ql_grouped", tag="ql_grouped", align_bytes=64)
            tok = slice(P * j, P * (j + 1))
            bank = new_bank()
            for t in range(4):
                feat = slice(P * (4 * g + t), P * (4 * g + t + 1))
                nc.tensor.matmul_mx(
                    out=bank[:, P * t : P * (t + 1)],
                    lhsT=wqa_codes[:, feat].bitcast(FP8X4), lhsT_scale=wqa_scales[:, feat],
                    rhs=h_codes[c][:, tok].bitcast(FP8X4), rhs_scale=h_scales[c][:, tok],
                    start=True, stop=True,
                )
            copy(
                out=ql_grouped[s][:, BANK * g : BANK * (g + 1)].rearrange("p (r t) -> p r t", t=4),
                in_=bank[:].rearrange("p (t r) -> p r t", t=4),
            )

        def q_lora_pair(q, copies=(scalar_copy, vector_copy, scalar_copy, vector_copy)):
            for i, copy in enumerate(copies):
                q_lora_bank(2 * q + i // 2, i % 2, copy)

        def q_lora_g(q, g, copies):
            for i, copy in enumerate(copies):
                q_lora_bank(2 * q + i, g, copy)

        def quantise_q_lora(s):
            ql_codes[s] = ql_code_pool.tile([P, 2 * P], U32, name="ql_codes", tag="ql_codes", align_bytes=64)
            ql_scales[s] = ql_code_pool.tile([P, 2 * P], U8, name="ql_scales", tag="ql_scales", align_bytes=64)
            quantise(ql_codes[s][:], ql_scales[s][:], ql_grouped[s][:])

        def dram_rows(c):
            return c // 2, slice(512 * (c % 2), 512 * (c % 2) + 512)

        def kv_pass(out, c, j, cols):
            tok = slice(P * j, P * (j + 1))
            nc.tensor.matmul_mx(
                out=out,
                lhsT=h_codes[c][:, tok].bitcast(FP8X4), lhsT_scale=h_scales[c][:, tok],
                rhs=wkv_codes[:, cols].bitcast(FP8X4), rhs_scale=wkv_scales[:, cols],
                start=True, stop=True,
            )

        chunk_kv = {}

        def kv_nope_pair(q):
            c, second = divmod(q, 2)
            batch, rows = dram_rows(c)
            if not second:
                chunk_kv[c] = kv_pool.tile([P, 4, NOPE], F32, name="kv_nope", tag="kv_nope")
            kv_nope = chunk_kv[c]
            kv_nope_bank = psum.tile([P, 2, NOPE], F32, name="bank", tag="bank")
            for i in range(2):
                kv_pass(kv_nope_bank[:, i, :], c, 2 * second + i, KV_NOPE)
            scalar_copy(out=kv_nope[:, 2 * second : 2 * second + 2, :], in_=kv_nope_bank[:])
            kv_dram = out_4[batch, rows, :].rearrange("(p j) f -> p j f", j=4)
            if c < 5:
                if second:
                    nc.sync.dma_start(out=kv_dram, in_=kv_nope[:])
            else:
                pair = slice(2 * second, 2 * second + 2)
                nc.sync.dma_start(out=kv_dram[:, pair, :], in_=kv_nope[:, pair, :])

        chunk_out = {}
        chunk_nope = {}

        def q_passes(out, s, codes, scales, width):
            for g in range(2):
                tok = slice(P * g, P * (g + 1))
                cols = slice(width * g, width * (g + 1))
                nc.tensor.matmul_mx(
                    out=out,
                    lhsT=ql_codes[s][:, tok].bitcast(FP8X4), lhsT_scale=ql_scales[s][:, tok],
                    rhs=codes[:, cols].bitcast(FP8X4), rhs_scale=scales[:, cols],
                    start=(g == 0), stop=(g == 1),
                )

        def rotate(out, x, tiles, heads, adder):
            count = tiles.stop - tiles.start
            by_cos = prod_pool.tile([P, count, heads, ROT], F32, name="by_cos", tag="by_cos%d" % heads)
            by_sin = prod_pool.tile([P, count, heads, ROT], F32, name="by_sin", tag="by_sin%d" % heads)
            for prod, table in ((by_cos, cos_sb), (by_sin, partner_sin)):
                nc.vector.tensor_tensor(
                    out=prod[:], in0=x, op=MULT,
                    in1=table[:, tiles, :].unsqueeze(2).to_broadcast([P, count, heads, ROT]),
                )
            for mine, partner in ((slice(0, 32), slice(32, 64)), (slice(32, 64), slice(0, 32))):
                adder.tensor_tensor(
                    out=out[:, :, :, mine],
                    in0=by_cos[:, :, :, mine].rearrange("p j n f -> p n j f"),
                    in1=by_sin[:, :, :, partner].rearrange("p j n f -> p n j f"),
                    op=ADD,
                )

        def kv_rot_chunk(c):
            batch, rows = dram_rows(c)
            bank = psum.tile([P, 4, 2 * ROT], F32, name="bank", tag="bank")
            for j in range(4):
                kv_pass(bank[:, j, :], c, j, KV_ROT)
            k_rope = out_pool.tile([P, 1, 4, ROT], F32, name="k_rope", tag="k_rope")
            v_rope = out_pool.tile([P, 4, ROT], F32, name="v_rope", tag="v_rope")
            rotate(k_rope, bank[:, :, 0:ROT].unsqueeze(2), slice(4 * c, 4 * c + 4), 1, nc.gpsimd)
            vector_copy(out=v_rope[:], in_=bank[:, :, ROT : 2 * ROT])
            nc.sync.dma_start(out=out_3[batch, rows, :].rearrange("(p j) f -> p j f", j=4), in_=v_rope[:])
            nc.sync.dma_start(out=out_2[batch, rows, :].rearrange("(p j) f -> p j f", j=4), in_=k_rope[:, 0, :, :])

        def rope_pair(q):
            c, second = divmod(q, 2)
            if not second:
                chunk_out[c] = out_pool.tile([P, 2, 4, ROT], F32, name="q_rope", tag="q_rope")
            bank = psum.tile([P, 2, 2, ROT], F32, name="bank", tag="bank")
            for i in range(2):
                q_passes(bank[:, i, :, :].rearrange("p n f -> p (n f)"), 2 * q + i, rot_codes, rot_scales, 2 * ROT)
            rotate(chunk_out[c][:, :, 2 * second : 2 * second + 2, :], bank[:], slice(2 * q, 2 * q + 2), 2, nc.vector if q == PAIRS - 1 else nc.gpsimd)

        def store_rope(q):
            c, second = divmod(q, 2)
            batch, rows = dram_rows(c)
            last_chunk = c == CHUNKS - 1
            if second:
                done = slice(0, 4)
                q_rope_dram = out_0[batch, :, rows, :].rearrange("h (p j) f -> p h j f", j=4)
                nc.sync.dma_start(out=q_rope_dram[:, :, done, :], in_=chunk_out[c][:, :, done, :])

        def nope_pair(q):
            c, second = divmod(q, 2)
            j0 = 2 * second
            pair = slice(j0, j0 + 2)
            batch, rows = dram_rows(c)
            if not second:
                chunk_nope[c] = q_nope_pool.tile([P, 2, 4, NOPE], F32, name="q_nope", tag="q_nope")
            q_nope = chunk_nope[c]
            q_nope_dram = out_1[batch, :, rows, :].rearrange("h (p j) f -> p h j f", j=4)
            for i in range(2):
                nope_bank = new_bank()
                q_passes(nope_bank[:], 2 * q + i, nope_codes, nope_scales, BANK)
                scalar_copy(out=q_nope[:, :, j0 + i, :], in_=nope_bank[:].rearrange("p (h f) -> p h f", h=2))
            if c < 5:
                if second:
                    nc.sync.dma_start(out=q_nope_dram, in_=q_nope[:])
            else:
                nc.sync.dma_start(out=q_nope_dram[:, :, pair, :], in_=q_nope[:, :, pair, :])

        V = vector_copy
        A = scalar_copy
        transpose_h(0, V)
        transpose_wqa(0, A)
        quantise_h(0)
        transpose_wqa(1, V)
        quantise_wqa(0)
        transpose_wqa(2, A)
        quantise_wqa(1)
        transpose_wqa(3, A)
        quantise_wqa(2)
        quantise_wqa(3)
        q_lora_g(0, 0, (A, V))
        q_lora_g(0, 1, (A, V))
        transpose_h(1, A)
        quantise_h(1)
        transpose_wqb(0, (A, V))
        quantise_q_lora(0)
        quantise_q_lora(1)
        transpose_wqb(2, (A, A, V))
        q_lora_g(1, 0, (A, A))
        quantise_nope(0)
        quantise_nope(1)
        q_lora_g(1, 1, (A, V))
        transpose_h(2, A)
        transpose_h(3, V)
        transpose_wkv()
        quantise_q_lora(2)
        quantise_q_lora(3)
        quantise_h_chunk(1)
        nope_pair(0)
        nope_pair(1)
        quantise_wkv()
        quantise_rot()
        q_lora_pair(2)
        prepare_sin(0)
        kv_nope_pair(0)
        rope_pair(0)
        kv_rot_chunk(0)
        quantise_q_lora(4)
        quantise_q_lora(5)
        transpose_h(4,A)
        transpose_h(5,A)
        rope_pair(1)
        store_rope(1)
        kv_nope_pair(1)
        kv_nope_pair(2)
        quantise_h_chunk(2)

        prepared = 2
        kv_done = 3
        kv_target = [min(PAIRS, q + 1 + (q - 3) // 2) for q in range(PAIRS + 3)]
        fresh = []
        for q in range(3, PAIRS + 1):
            new = range(prepared + 1, (kv_target[q + 2] - 1) // 2 + 1)
            for c in new:
                transpose_h(2 * c, A)
                transpose_h(2 * c + 1, A)
            if q < PAIRS:
                q_lora_pair(q)
                quantise_q_lora(2 * q)
                quantise_q_lora(2 * q + 1)
            for c in fresh:
                quantise_h_chunk(c)
            fresh = new
            for p in range(kv_done, kv_target[q]):
                kv_nope_pair(p)
            rope_pair(q - 1)
            nope_pair(q - 1)
            store_rope(q - 1)
            for p in range(kv_done, kv_target[q]):
                if p % 2:
                    kv_rot_chunk(p // 2)
            kv_done = kv_target[q]
            for c in new:
                prepared = c
                if c == 4:
                    prepare_sin(1)
